import numpy as np
import ml_dtypes


def mxq(x, axis, fmt="e4m3"):
    dtype, down = {"e4m3": (ml_dtypes.float8_e4m3fn, 7), "e5m2": (ml_dtypes.float8_e5m2, 14)}[fmt]
    v = np.moveaxis(np.asarray(x, np.float32).astype(ml_dtypes.bfloat16).astype(np.float64), axis, -1)
    blocks = v.reshape(v.shape[:-1] + (-1, 32))
    amax = np.abs(blocks).max(-1, keepdims=True)
    byte = np.maximum(np.where(amax > 0, np.frexp(amax)[1] - 1 + 127, 0) - down, 1)
    scale = np.exp2(byte - 127.0)
    codes = (blocks / scale).astype(np.float32).astype(dtype).astype(np.float64)
    return np.moveaxis((codes * scale).reshape(v.shape), -1, axis)


WIDE = False


def mx_kscale(k):
    if not WIDE:
        return np.ones(k)
    levels = np.array([10, -10, 5, -5, 0])
    if k % 512:
        return np.exp2(np.random.permutation(np.resize(levels, k // 32))).repeat(32)
    a = np.empty((k // 512, 16))
    for p in range(k // 512):
        a[p, :8] = np.random.permutation(np.resize(levels, 8))
        for g in range(8):
            far = levels[np.abs(levels - a[p, g]) >= 10]
            a[p, g + 8] = far[np.random.randint(len(far))]
    return np.exp2(a.ravel()).repeat(32)


BF16 = ml_dtypes.bfloat16


def bf(x):
    return np.asarray(x, np.float32).astype(BF16)


def f64(x):
    return np.asarray(x).astype(np.float64)


B, S, D, NQ, NKV, H, WINDOW, QB = 1, 1024, 1024, 8, 4, 256, 512, 512
HALF = H // 2
MAX_WAVELENGTH = 10000.0


def rope_interleaved(u):
    inv_freq = 1.0 / MAX_WAVELENGTH ** (np.arange(0, H, 2) / H)
    freq = np.arange(S)[:, None] * inv_freq[None, :]
    cos = np.cos(freq)[None, :, None, :]
    sin = np.sin(freq)[None, :, None, :]
    u1, u2 = u[..., :HALF], u[..., HALF:]
    r1 = u1 * cos - u2 * sin
    r2 = u2 * cos + u1 * sin
    return np.stack([r1, r2], axis=-1).reshape(u.shape)


def draw0():
    s = mx_kscale(D)
    return {"x": bf(np.random.standard_normal((B, S, D)) * s),
            "Wq": bf(np.random.standard_normal((NQ, D, H)) * 2.5 / np.sqrt(D) / s[None, :, None]),
            "Wk": bf(np.random.standard_normal((NKV, D, H)) * 2.5 / np.sqrt(D) / s[None, :, None])}


def core(x, Wq, Wk):
    xq = mxq(f64(x), 2, "e4m3")
    uq = (xq[:, None] @ mxq(f64(Wq), 1, "e4m3")[None]).transpose(0, 2, 1, 3)
    uk = (xq[:, None] @ mxq(f64(Wk), 1, "e4m3")[None]).transpose(0, 2, 1, 3)
    q = rope_interleaved(uq) * (1.0 / np.sqrt(H))
    k = rope_interleaved(uk)
    return q, k


def e4m3fn_bytes(y):
    return np.clip(np.asarray(y, np.float64), -448.0, 448.0).astype(np.float32).astype(ml_dtypes.float8_e4m3fn).view(np.uint8)


def e4m3fn_values(b):
    return np.asarray(b, np.uint8).view(ml_dtypes.float8_e4m3fn).astype(np.float64)


def setup_inputs():
    d = draw0()
    x0 = np.asarray(d['Wq']).astype(np.float64)
    s = (np.max(np.abs(x0), axis=(0, 2), keepdims=True) / 448.0).astype(np.float32)
    out = {}
    for k, v in d.items():
        if k == 'Wq':
            out['Wq_bytes'] = e4m3fn_bytes(x0 / s.astype(np.float64))
            out['Wq_scale'] = s
        else:
            out[k] = v
    return out


def reference(x, Wq_bytes, Wq_scale, Wk):
    return core(x, e4m3fn_values(Wq_bytes) * Wq_scale.astype(np.float64), Wk)

@@ -1,0 +1,206 @@
+import math
+from contextlib import ExitStack
+
+import concourse.mybir as mybir
+from concourse.masks import make_identity
+
+S_LEN, D, NQ, NKV, H = 1024, 1024, 8, 4, 256
+HALF = H // 2
+FLOPS = 2 * S_LEN * D * (NQ + NKV) * H
+
+F32 = mybir.dt.float32
+BF16 = mybir.dt.bfloat16
+U32 = mybir.dt.uint32
+U8 = mybir.dt.uint8
+I32 = mybir.dt.int32
+FP8 = mybir.dt.float8_e4m3fn
+FP8X4 = mybir.dt.float8_e4m3fn_x4
+ALU = mybir.AluOpType
+ACT = mybir.ActivationFunctionType
+
+P = 128
+NT = S_LEN // P
+NG = D // 512
+CH = 2
+CHUNKS = (("k", 0), ("k", 2), ("q", 0), ("q", 2), ("q", 4), ("q", 6))
+
+
+def tile_gemma2attention_pa_kernel(tc, x, Wq_bytes, Wq_scale, Wk, out_0, out_1):
+    nc = tc.nc
+    with ExitStack() as ctx:
+        keep = ctx.enter_context(tc.tile_pool(name="keep", bufs=1))
+        stage = ctx.enter_context(tc.tile_pool(name="stage", bufs=2))
+        work = ctx.enter_context(tc.tile_pool(name="work", bufs=4))
+        psum = ctx.enter_context(tc.psum_pool(name="psum", bufs=2))
+
+        raw = {}
+        for j, (kind, n0) in enumerate(CHUNKS):
+            if kind == "k":
+                raw[j] = keep.tile([P, NG, CH, 4, H], BF16, name="wk_raw%d" % j)
+            else:
+                raw[j] = keep.tile([P, NG, CH, 4, H], U8, name="wq_bytes%d" % j)
+
+        def load_w(j):
+            kind, n0 = CHUNKS[j]
+            src = Wk if kind == "k" else Wq_bytes
+            view = src[n0 : n0 + CH].rearrange("n (g p t) c -> g p n (t c)", g=NG, p=P, t=4)
+            for g in range(NG):
+                nc.sync.dma_start(out=raw[j][:, g].rearrange("p n t c -> p n (t c)"), in_=view[g])
+
+        x_sb = []
+        x_view = x[0].rearrange("(a p) k -> a p k", p=P)
+        load_w(0)
+        for a in range(NT):
+            xt_sb = keep.tile([P, D], BF16, name="x_sb%d" % a)
+            nc.sync.dma_start(out=xt_sb[:], in_=x_view[a])
+            x_sb.append(xt_sb)
+        wscale = keep.tile([P, NG, 4], F32, name="wscale")
+        nc.sync.dma_start(out=wscale[:], in_=Wq_scale.rearrange("o (g p t) z -> p (o g) (t z)", g=NG, p=P, t=4))
+        for j in range(1, len(CHUNKS)):
+            load_w(j)
+
+        warm = keep.tile([P, 1], F32, name="warm")
+        nc.vector.memset(warm[:], 0.0)
+        nc.scalar.activation(out=warm[:], in_=warm[:], func=ACT.Sin)
+
+        ident = keep.tile([P, P], F32, name="ident")
+        make_identity(nc, ident[:])
+
+        tok_i = keep.tile([P, NT], I32, name="tok_i")
+        nc.gpsimd.iota(tok_i[:], pattern=[[P, NT]], base=0, channel_multiplier=1)
+        tok_f = keep.tile([P, NT], F32, name="tok_f")
+        nc.vector.tensor_copy(out=tok_f[:], in_=tok_i[:])
+
+        freq = keep.tile([P, HALF], F32, name="freq")
+        nc.vector.memset(freq[:], 1.0)
+        nc.vector.tensor_scalar(out=freq[:], in0=freq[:], scalar1=1.0 / (2.0 * math.pi), scalar2=None, op0=ALU.mult)
+        for b in range(7):
+            sel = freq[:].rearrange("p (a two l) -> p a two l", two=2, l=2**b)[:, :, 1, :]
+            nc.vector.tensor_scalar(out=sel, in0=sel, scalar1=10000.0 ** (-(2.0**b) / HALF), scalar2=None, op0=ALU.mult)
+
+        turns = keep.tile([P, NT, HALF], F32, name="turns")
+        nc.vector.tensor_tensor(
+            out=turns[:],
+            in0=freq[:].unsqueeze(1).to_broadcast([P, NT, HALF]),
+            in1=tok_f[:].unsqueeze(2).to_broadcast([P, NT, HALF]),
+            op=ALU.mult,
+        )
+        whole = keep.tile([P, NT, HALF], I32, name="whole")
+        nc.vector.tensor_copy(out=whole[:], in_=turns[:])
+        frac = keep.tile([P, NT, HALF], F32, name="frac")
+        nc.vector.tensor_tensor(out=frac[:], in0=turns[:], in1=whole[:], op=ALU.subtract)
+        afrac = keep.tile([P, NT, HALF], F32, name="afrac")
+        nc.scalar.activation(out=afrac[:], in_=frac[:], func=ACT.Abs)
+        tb = keep.tile([P, NT, 3, HALF], F32, name="tb")
+        two_pi = 2.0 * math.pi
+        nc.scalar.activation(out=tb[:, :, 1, :], in_=afrac[:], func=ACT.Sin, scale=-two_pi, bias=math.pi / 2.0)
+        nc.scalar.activation(out=tb[:, :, 2, :], in_=frac[:], func=ACT.Sin, scale=two_pi)
+        nc.scalar.activation(out=tb[:, :, 0, :], in_=frac[:], func=ACT.Sin, scale=-two_pi)
+        tbq = keep.tile([P, NT, 3, HALF], F32, name="tbq")
+        nc.gpsimd.tensor_scalar(out=tbq[:], in0=tb[:], scalar1=1.0 / math.sqrt(H), scalar2=0.0, op0=ALU.mult, op1=ALU.add)
+
+        x_codes = keep.tile([P, NT, NG * P], U32, name="x_codes", align_bytes=64)
+        x_scales = keep.tile([P, NT, NG * P], U8, name="x_scales", align_bytes=64)
+
+        def prep_x(a):
+            words = x_sb[a][:].bitcast(F32)
+            xt = psum.tile([P, NG, 2, P], F32, name="xt", tag="xt", bufs=2)
+            for g in range(NG):
+                for u in range(2):
+                    nc.tensor.transpose(xt[:, g, u, :], words[:, 256 * g + u : 256 * (g + 1) : 2], ident[:])
+            xg = stage.tile([P, NG, P, 4], BF16, name="xg", tag="xg", bufs=3, align_bytes=64)
+            nc.scalar.copy(out=xg[:].bitcast(F32), in_=xt[:].rearrange("p g u r -> p g r u"))
+            nc.vector.quantize_mx(
+                out=x_codes[:, a, :].bitcast(FP8X4),
+                scales=x_scales[:, a, :],
+                in_=xg[:].rearrange("p g r j -> p (g r j)"),
+            )
+
+        w_codes = {}
+        w_scales = {}
+        w_grouped = {}
+
+        def prep_w_copy(j, on_vector):
+            kind, n0 = CHUNKS[j]
+            if kind == "k":
+                src = raw[j]
+            else:
+                src = stage.tile([P, NG, CH, 4, H], BF16, name="wide", tag="wide", bufs=2)
+                for g in range(NG):
+                    for n in range(CH):
+                        for t in range(4):
+                            nc.scalar.activation(
+                                out=src[:, g, n, t, :],
+                                in_=raw[j][:, g, n, t, :].bitcast(FP8),
+                                func=ACT.Copy,
+                                scale=wscale[:, g, t : t + 1],
+                            )
+            wg = stage.tile([P, NG * CH, H, 4], BF16, name="wg", tag="wg", bufs=2, align_bytes=64)
+            view = src[:].rearrange("p g n t c -> p (g n) c t")
+            if on_vector:
+                for g in range(NG):
+                    nc.vector.tensor_copy(out=wg[:, g * CH : (g + 1) * CH], in_=view[:, g * CH : (g + 1) * CH])
+            else:
+                nc.scalar.copy(out=wg[:], in_=view)
+            w_grouped[j] = wg
+
+        def prep_w_quant(j):
+            w_codes[j] = keep.tile([P, NG * CH * H], U32, name="w_codes%d" % j, align_bytes=64)
+            w_scales[j] = keep.tile([P, NG * CH * H], U8, name="w_scales%d" % j, align_bytes=64)
+            nc.vector.quantize_mx(
+                out=w_codes[j][:].bitcast(FP8X4),
+                scales=w_scales[j][:],
+                in_=w_grouped[j][:].rearrange("p a c t -> p (a c t)"),
+            )
+
+        def rope(j, a):
+            kind, n0 = CHUNKS[j]
+            table = tb if kind == "k" else tbq
+            dst = out_1 if kind == "k" else out_0
+            width = CH * H
+            acc = psum.tile([P, width], F32, name="acc", tag="acc", bufs=6)
+            for g in range(NG):
+                nc.tensor.matmul_mx(
+                    out=acc[:],
+                    lhsT=x_codes[:, a, g * P : (g + 1) * P].bitcast(FP8X4),
+                    lhsT_scale=x_scales[:, a, g * P : (g + 1) * P],
+                    rhs=w_codes[j][:, g * width : (g + 1) * width].bitcast(FP8X4),
+                    rhs_scale=w_scales[j][:, g * width : (g + 1) * width],
+                    start=(g == 0),
+                    stop=(g == NG - 1),
+                )
+            halves = acc[:].rearrange("p (h e i) -> p h e i", h=CH, e=2)
+            shape = [P, CH, HALF, 2]
+            first = work.tile([P, width], F32, name="first", tag="first")
+            second = work.tile([P, width], F32, name="second", tag="second")
+            nc.vector.tensor_tensor(
+                out=first[:].rearrange("p (h i e) -> p h i e", h=CH, e=2),
+                in0=halves[:, :, 0, :].unsqueeze(3).to_broadcast(shape),
+                in1=table[:, a, 1:3, :].rearrange("p e i -> p i e").unsqueeze(1).to_broadcast(shape),
+                op=ALU.mult,
+            )
+            nc.vector.tensor_tensor(
+                out=second[:].rearrange("p (h i e) -> p h i e", h=CH, e=2),
+                in0=halves[:, :, 1, :].unsqueeze(3).to_broadcast(shape),
+                in1=table[:, a, 0:2, :].rearrange("p e i -> p i e").unsqueeze(1).to_broadcast(shape),
+                op=ALU.mult,
+            )
+            res = work.tile([P, width], F32, name="res", tag="res")
+            nc.gpsimd.tensor_tensor(out=res[:], in0=first[:], in1=second[:], op=ALU.add)
+            nc.sync.dma_start(
+                out=dst[0, a * P : (a + 1) * P, n0 : n0 + CH, :],
+                in_=res[:].rearrange("p (h c) -> p h c", h=CH),
+            )
+
+        prep_w_copy(0, True)
+        prep_w_quant(0)
+        for a in range(NT):
+            prep_x(a)
+        prep_w_copy(1, False)
+        for j in range(len(CHUNKS)):
+            for a in range(NT):
+                rope(j, a)
+                if a == 1 and j + 2 < len(CHUNKS):
+                    prep_w_copy(j + 2, False)
+                if a == 5 and j + 1 < len(CHUNKS):
+                    prep_w_quant(j + 1)

@@ -79,25 +79,30 @@ def tile_gemma2attention_pa_kernel(tc, x, Wq_bytes, Wq_scale, Wk, out_0, out_1):
             nc.vector.tensor_scalar(out=sel, in0=sel, scalar1=10000.0 ** (-(2.0**b) / HALF), scalar2=None, op0=ALU.mult)
 
         turns = keep.tile([P, NT, HALF], F32, name="turns")
-        nc.vector.tensor_tensor(
-            out=turns[:],
-            in0=freq[:].unsqueeze(1).to_broadcast([P, NT, HALF]),
-            in1=tok_f[:].unsqueeze(2).to_broadcast([P, NT, HALF]),
-            op=ALU.mult,
-        )
         whole = keep.tile([P, NT, HALF], I32, name="whole")
-        nc.vector.tensor_copy(out=whole[:], in_=turns[:])
         frac = keep.tile([P, NT, HALF], F32, name="frac")
-        nc.vector.tensor_tensor(out=frac[:], in0=turns[:], in1=whole[:], op=ALU.subtract)
         afrac = keep.tile([P, NT, HALF], F32, name="afrac")
-        nc.scalar.activation(out=afrac[:], in_=frac[:], func=ACT.Abs)
         tb = keep.tile([P, NT, 3, HALF], F32, name="tb")
-        two_pi = 2.0 * math.pi
-        nc.scalar.activation(out=tb[:, :, 1, :], in_=afrac[:], func=ACT.Sin, scale=-two_pi, bias=math.pi / 2.0)
-        nc.scalar.activation(out=tb[:, :, 2, :], in_=frac[:], func=ACT.Sin, scale=two_pi)
-        nc.scalar.activation(out=tb[:, :, 0, :], in_=frac[:], func=ACT.Sin, scale=-two_pi)
         tbq = keep.tile([P, NT, 3, HALF], F32, name="tbq")
-        nc.gpsimd.tensor_scalar(out=tbq[:], in0=tb[:], scalar1=1.0 / math.sqrt(H), scalar2=0.0, op0=ALU.mult, op1=ALU.add)
+        two_pi = 2.0 * math.pi
+
+        def make_tables(a0, a1):
+            n = a1 - a0
+            nc.vector.tensor_tensor(
+                out=turns[:, a0:a1],
+                in0=freq[:].unsqueeze(1).to_broadcast([P, n, HALF]),
+                in1=tok_f[:, a0:a1].unsqueeze(2).to_broadcast([P, n, HALF]),
+                op=ALU.mult,
+            )
+            nc.vector.tensor_copy(out=whole[:, a0:a1], in_=turns[:, a0:a1])
+            nc.vector.tensor_tensor(out=frac[:, a0:a1], in0=turns[:, a0:a1], in1=whole[:, a0:a1], op=ALU.subtract)
+            nc.scalar.activation(out=afrac[:, a0:a1], in_=frac[:, a0:a1], func=ACT.Abs)
+            nc.scalar.activation(out=tb[:, a0:a1, 1, :], in_=afrac[:, a0:a1], func=ACT.Sin, scale=-two_pi, bias=math.pi / 2.0)
+            nc.scalar.activation(out=tb[:, a0:a1, 2, :], in_=frac[:, a0:a1], func=ACT.Sin, scale=two_pi)
+            nc.scalar.activation(out=tb[:, a0:a1, 0, :], in_=frac[:, a0:a1], func=ACT.Sin, scale=-two_pi)
+
+        make_tables(0, 2)
+        make_tables(2, NT)
 
         x_codes = keep.tile([P, NT, NG * P], U32, name="x_codes", align_bytes=64)
         x_scales = keep.tile([P, NT, NG * P], U8, name="x_scales", align_bytes=64)
@@ -153,11 +158,12 @@ def tile_gemma2attention_pa_kernel(tc, x, Wq_bytes, Wq_scale, Wk, out_0, out_1):
                 in_=w_grouped[j][:].rearrange("p a c t -> p (a c t)"),
             )
 
-        def rope(j, a):
+        width = CH * H
+        shape = [P, CH, HALF, 2]
+
+        def products(j, a, first, second):
             kind, n0 = CHUNKS[j]
             table = tb if kind == "k" else tbq
-            dst = out_1 if kind == "k" else out_0
-            width = CH * H
             acc = psum.tile([P, width], F32, name="acc", tag="acc", bufs=6)
             for g in range(NG):
                 nc.tensor.matmul_mx(
@@ -170,26 +176,31 @@ def tile_gemma2attention_pa_kernel(tc, x, Wq_bytes, Wq_scale, Wk, out_0, out_1):
                     stop=(g == NG - 1),
                 )
             halves = acc[:].rearrange("p (h e i) -> p h e i", h=CH, e=2)
-            shape = [P, CH, HALF, 2]
-            first = work.tile([P, width], F32, name="first", tag="first")
-            second = work.tile([P, width], F32, name="second", tag="second")
             nc.vector.tensor_tensor(
-                out=first[:].rearrange("p (h i e) -> p h i e", h=CH, e=2),
-                in0=halves[:, :, 0, :].unsqueeze(3).to_broadcast(shape),
-                in1=table[:, a, 1:3, :].rearrange("p e i -> p i e").unsqueeze(1).to_broadcast(shape),
+                out=first.rearrange("p (h i e) -> p h i e", h=CH, e=2),
+                in0=table[:, a, 1:3, :].rearrange("p e i -> p i e").unsqueeze(1).to_broadcast(shape),
+                in1=halves[:, :, 0, :].unsqueeze(3).to_broadcast(shape),
                 op=ALU.mult,
             )
             nc.vector.tensor_tensor(
-                out=second[:].rearrange("p (h i e) -> p h i e", h=CH, e=2),
-                in0=halves[:, :, 1, :].unsqueeze(3).to_broadcast(shape),
-                in1=table[:, a, 0:2, :].rearrange("p e i -> p i e").unsqueeze(1).to_broadcast(shape),
+                out=second.rearrange("p (h i e) -> p h i e", h=CH, e=2),
+                in0=table[:, a, 0:2, :].rearrange("p e i -> p i e").unsqueeze(1).to_broadcast(shape),
+                in1=halves[:, :, 1, :].unsqueeze(3).to_broadcast(shape),
                 op=ALU.mult,
             )
-            res = work.tile([P, width], F32, name="res", tag="res")
-            nc.gpsimd.tensor_tensor(out=res[:], in0=first[:], in1=second[:], op=ALU.add)
+
+        def rope(j, a0, count, add_engine):
+            kind, n0 = CHUNKS[j]
+            dst = out_1 if kind == "k" else out_0
+            first = work.tile([P, 2, width], F32, name="first", tag="first", bufs=3)
+            second = work.tile([P, 2, width], F32, name="second", tag="second", bufs=3)
+            res = work.tile([P, 2, width], F32, name="res", tag="res", bufs=6)
+            for b in range(count):
+                products(j, a0 + b, first[:, b, :], second[:, b, :])
+            add_engine.tensor_tensor(out=res[:, 0:count, :], in0=first[:, 0:count, :], in1=second[:, 0:count, :], op=ALU.add)
             nc.sync.dma_start(
-                out=dst[0, a * P : (a + 1) * P, n0 : n0 + CH, :],
-                in_=res[:].rearrange("p (h c) -> p h c", h=CH),
+                out=dst[0, a0 * P : (a0 + count) * P, n0 : n0 + CH, :].rearrange("(b p) h c -> p b (h c)", p=P),
+                in_=res[:, 0:count, :],
             )
 
         prep_w_copy(0, True)
@@ -197,10 +208,16 @@ def tile_gemma2attention_pa_kernel(tc, x, Wq_bytes, Wq_scale, Wk, out_0, out_1):
         for a in range(NT):
             prep_x(a)
         prep_w_copy(1, False)
+        nc.scalar.mul(tbq[:], tb[:], 1.0 / math.sqrt(H))
+        last = len(CHUNKS) - 1
         for j in range(len(CHUNKS)):
-            for a in range(NT):
-                rope(j, a)
-                if a == 1 and j + 2 < len(CHUNKS):
+            for a0 in range(0, NT, 2):
+                if j == last and a0 == NT - 2:
+                    rope(j, a0, 1, nc.gpsimd)
+                    rope(j, a0 + 1, 1, nc.vector)
+                else:
+                    rope(j, a0, 2, nc.gpsimd)
+                if a0 == 0 and j + 2 < len(CHUNKS):
                     prep_w_copy(j + 2, False)
-                if a == 5 and j + 1 < len(CHUNKS):
+                if a0 == 4 and j + 1 < len(CHUNKS):
                     prep_w_quant(j + 1)

@@ -78,28 +78,32 @@ def tile_gemma2attention_pa_kernel(tc, x, Wq_bytes, Wq_scale, Wk, out_0, out_1):
             sel = freq[:].rearrange("p (a two l) -> p a two l", two=2, l=2**b)[:, :, 1, :]
             nc.vector.tensor_scalar(out=sel, in0=sel, scalar1=10000.0 ** (-(2.0**b) / HALF), scalar2=None, op0=ALU.mult)
 
-        turns = keep.tile([P, NT, HALF], F32, name="turns")
-        whole = keep.tile([P, NT, HALF], I32, name="whole")
-        frac = keep.tile([P, NT, HALF], F32, name="frac")
-        afrac = keep.tile([P, NT, HALF], F32, name="afrac")
         tb = keep.tile([P, NT, 3, HALF], F32, name="tb")
         tbq = keep.tile([P, NT, 3, HALF], F32, name="tbq")
         two_pi = 2.0 * math.pi
 
         def make_tables(a0, a1):
             n = a1 - a0
+            turns = keep.tile([P, n, HALF], F32, name="turns%d" % a0)
+            whole = keep.tile([P, n, HALF], I32, name="whole%d" % a0)
+            frac = keep.tile([P, n, HALF], F32, name="frac%d" % a0)
+            afrac = keep.tile([P, n, HALF], F32, name="afrac%d" % a0)
+            sin_t = keep.tile([P, n, HALF], F32, name="sin_t%d" % a0)
+            msin_t = keep.tile([P, n, HALF], F32, name="msin_t%d" % a0)
             nc.vector.tensor_tensor(
-                out=turns[:, a0:a1],
+                out=turns[:],
                 in0=freq[:].unsqueeze(1).to_broadcast([P, n, HALF]),
                 in1=tok_f[:, a0:a1].unsqueeze(2).to_broadcast([P, n, HALF]),
                 op=ALU.mult,
             )
-            nc.vector.tensor_copy(out=whole[:, a0:a1], in_=turns[:, a0:a1])
-            nc.vector.tensor_tensor(out=frac[:, a0:a1], in0=turns[:, a0:a1], in1=whole[:, a0:a1], op=ALU.subtract)
-            nc.scalar.activation(out=afrac[:, a0:a1], in_=frac[:, a0:a1], func=ACT.Abs)
-            nc.scalar.activation(out=tb[:, a0:a1, 1, :], in_=afrac[:, a0:a1], func=ACT.Sin, scale=-two_pi, bias=math.pi / 2.0)
-            nc.scalar.activation(out=tb[:, a0:a1, 2, :], in_=frac[:, a0:a1], func=ACT.Sin, scale=two_pi)
-            nc.scalar.activation(out=tb[:, a0:a1, 0, :], in_=frac[:, a0:a1], func=ACT.Sin, scale=-two_pi)
+            nc.vector.tensor_copy(out=whole[:], in_=turns[:])
+            nc.vector.tensor_tensor(out=frac[:], in0=turns[:], in1=whole[:], op=ALU.subtract)
+            nc.scalar.activation(out=afrac[:], in_=frac[:], func=ACT.Abs)
+            nc.scalar.activation(out=tb[:, a0:a1, 2, :], in_=afrac[:], func=ACT.Sin, scale=-two_pi, bias=math.pi / 2.0)
+            nc.scalar.activation(out=msin_t[:], in_=frac[:], func=ACT.Sin, scale=-two_pi)
+            nc.scalar.activation(out=sin_t[:], in_=frac[:], func=ACT.Sin, scale=two_pi)
+            nc.gpsimd.tensor_tensor(out=tb[:, a0:a1, 0, :], in0=msin_t[:], in1=tb[:, a0:a1, 2, :], op=ALU.subtract)
+            nc.gpsimd.tensor_tensor(out=tb[:, a0:a1, 1, :], in0=sin_t[:], in1=tb[:, a0:a1, 2, :], op=ALU.subtract)
 
         make_tables(0, 2)
         make_tables(2, NT)
@@ -140,13 +144,14 @@ def tile_gemma2attention_pa_kernel(tc, x, Wq_bytes, Wq_scale, Wk, out_0, out_1):
                                 func=ACT.Copy,
                                 scale=wscale[:, g, t : t + 1],
                             )
-            wg = stage.tile([P, NG * CH, H, 4], BF16, name="wg", tag="wg", bufs=2, align_bytes=64)
-            view = src[:].rearrange("p g n t c -> p (g n) c t")
-            if on_vector:
-                for g in range(NG):
-                    nc.vector.tensor_copy(out=wg[:, g * CH : (g + 1) * CH], in_=view[:, g * CH : (g + 1) * CH])
-            else:
-                nc.scalar.copy(out=wg[:], in_=view)
+            wg = stage.tile([P, NG, 2, CH, HALF, 4], BF16, name="wg", tag="wg", bufs=2, align_bytes=64)
+            for g in range(NG):
+                for e in range(2):
+                    view = src[:, g, :, :, e * HALF : (e + 1) * HALF].rearrange("p h t i -> p h i t")
+                    if on_vector:
+                        nc.vector.tensor_copy(out=wg[:, g, 1 - e], in_=view)
+                    else:
+                        nc.scalar.copy(out=wg[:, g, 1 - e], in_=view)
             w_grouped[j] = wg
 
         def prep_w_quant(j):
@@ -155,49 +160,57 @@ def tile_gemma2attention_pa_kernel(tc, x, Wq_bytes, Wq_scale, Wk, out_0, out_1):
             nc.vector.quantize_mx(
                 out=w_codes[j][:].bitcast(FP8X4),
                 scales=w_scales[j][:],
-                in_=w_grouped[j][:].rearrange("p a c t -> p (a c t)"),
+                in_=w_grouped[j][:].rearrange("p g e h i t -> p (g e h i t)"),
             )
 
         width = CH * H
-        shape = [P, CH, HALF, 2]
+        half_w = CH * HALF
 
-        def products(j, a, first, second):
-            kind, n0 = CHUNKS[j]
-            table = tb if kind == "k" else tbq
-            acc = psum.tile([P, width], F32, name="acc", tag="acc", bufs=6)
-            for g in range(NG):
-                nc.tensor.matmul_mx(
-                    out=acc[:],
-                    lhsT=x_codes[:, a, g * P : (g + 1) * P].bitcast(FP8X4),
-                    lhsT_scale=x_scales[:, a, g * P : (g + 1) * P],
-                    rhs=w_codes[j][:, g * width : (g + 1) * width].bitcast(FP8X4),
-                    rhs_scale=w_scales[j][:, g * width : (g + 1) * width],
-                    start=(g == 0),
-                    stop=(g == NG - 1),
-                )
-            halves = acc[:].rearrange("p (h e i) -> p h e i", h=CH, e=2)
-            nc.vector.tensor_tensor(
-                out=first.rearrange("p (h i e) -> p h i e", h=CH, e=2),
-                in0=table[:, a, 1:3, :].rearrange("p e i -> p i e").unsqueeze(1).to_broadcast(shape),
-                in1=halves[:, :, 0, :].unsqueeze(3).to_broadcast(shape),
-                op=ALU.mult,
-            )
-            nc.vector.tensor_tensor(
-                out=second.rearrange("p (h i e) -> p h i e", h=CH, e=2),
-                in0=table[:, a, 0:2, :].rearrange("p e i -> p i e").unsqueeze(1).to_broadcast(shape),
-                in1=halves[:, :, 1, :].unsqueeze(3).to_broadcast(shape),
-                op=ALU.mult,
+        def mx(out, j, a, g, c0, c1, start, stop):
+            nc.tensor.matmul_mx(
+                out=out,
+                lhsT=x_codes[:, a, g * P : (g + 1) * P].bitcast(FP8X4),
+                lhsT_scale=x_scales[:, a, g * P : (g + 1) * P],
+                rhs=w_codes[j][:, g * width + c0 : g * width + c1].bitcast(FP8X4),
+                rhs_scale=w_scales[j][:, g * width + c0 : g * width + c1],
+                start=start,
+                stop=stop,
             )
 
         def rope(j, a0, count, add_engine):
             kind, n0 = CHUNKS[j]
+            table = tb if kind == "k" else tbq
             dst = out_1 if kind == "k" else out_0
-            first = work.tile([P, 2, width], F32, name="first", tag="first", bufs=3)
-            second = work.tile([P, 2, width], F32, name="second", tag="second", bufs=3)
+            side = work.tile([P, 2, width], F32, name="side", tag="side", bufs=3)
+            mid = work.tile([P, 2, half_w], F32, name="mid", tag="mid", bufs=3)
             res = work.tile([P, 2, width], F32, name="res", tag="res", bufs=6)
+            both = psum.tile([P, 2, half_w], F32, name="both", tag="both", bufs=2)
             for b in range(count):
-                products(j, a0 + b, first[:, b, :], second[:, b, :])
-            add_engine.tensor_tensor(out=res[:, 0:count, :], in0=first[:, 0:count, :], in1=second[:, 0:count, :], op=ALU.add)
+                a = a0 + b
+                acc = psum.tile([P, width], F32, name="acc", tag="acc", bufs=4)
+                for g in range(NG):
+                    mx(acc[:], j, a, g, 0, width, g == 0, g == NG - 1)
+                for g in range(NG):
+                    for e in range(2):
+                        mx(both[:, b, :], j, a, g, e * half_w, (e + 1) * half_w, g == 0 and e == 0, g == NG - 1 and e == 1)
+                nc.vector.tensor_tensor(
+                    out=side[:, b, :].rearrange("p (h i e) -> p h i e", h=CH, e=2),
+                    in0=table[:, a, 0:2, :].rearrange("p e i -> p i e").unsqueeze(1).to_broadcast([P, CH, HALF, 2]),
+                    in1=acc[:].rearrange("p (e h i) -> p h i e", e=2, h=CH),
+                    op=ALU.mult,
+                )
+            nc.vector.tensor_tensor(
+                out=mid[:, 0:count, :].rearrange("p b (h i) -> p b h i", h=CH),
+                in0=table[:, a0 : a0 + count, 2, :].unsqueeze(2).to_broadcast([P, count, CH, HALF]),
+                in1=both[:, 0:count, :].rearrange("p b (h i) -> p b h i", h=CH),
+                op=ALU.mult,
+            )
+            add_engine.tensor_tensor(
+                out=res[:, 0:count, :].rearrange("p b (c e) -> p (b c) e", e=2),
+                in0=side[:, 0:count, :].rearrange("p b (c e) -> p (b c) e", e=2),
+                in1=mid[:, 0:count, :].rearrange("p b c -> p (b c)").unsqueeze(2).to_broadcast([P, count * half_w, 2]),
+                op=ALU.add,
+            )
             nc.sync.dma_start(
                 out=dst[0, a0 * P : (a0 + count) * P, n0 : n0 + CH, :].rearrange("(b p) h c -> p b (h c)", p=P),
                 in_=res[:, 0:count, :],

@@ -32,6 +32,7 @@ def tile_gemma2attention_pa_kernel(tc, x, Wq_bytes, Wq_scale, Wk, out_0, out_1):
         stage = ctx.enter_context(tc.tile_pool(name="stage", bufs=2))
         work = ctx.enter_context(tc.tile_pool(name="work", bufs=4))
         psum = ctx.enter_context(tc.psum_pool(name="psum", bufs=2))
+        ctx.enter_context(tc.manual_schedule(engines={mybir.EngineType.DVE}))
 
         raw = {}
         for j, (kind, n0) in enumerate(CHUNKS):
@@ -63,11 +64,10 @@ def tile_gemma2attention_pa_kernel(tc, x, Wq_bytes, Wq_scale, Wk, out_0, out_1):
         nc.vector.memset(warm[:], 0.0)
         nc.scalar.activation(out=warm[:], in_=warm[:], func=ACT.Sin)
 
-        ident = keep.tile([P, P], F32, name="ident")
-        make_identity(nc, ident[:])
-
         tok_i = keep.tile([P, NT], I32, name="tok_i")
         nc.gpsimd.iota(tok_i[:], pattern=[[P, NT]], base=0, channel_multiplier=1)
+        ident = keep.tile([P, P], F32, name="ident")
+        make_identity(nc, ident[:])
         tok_f = keep.tile([P, NT], F32, name="tok_f")
         nc.vector.tensor_copy(out=tok_f[:], in_=tok_i[:])
 
@@ -102,8 +102,9 @@ def tile_gemma2attention_pa_kernel(tc, x, Wq_bytes, Wq_scale, Wk, out_0, out_1):
             nc.scalar.activation(out=tb[:, a0:a1, 2, :], in_=afrac[:], func=ACT.Sin, scale=-two_pi, bias=math.pi / 2.0)
             nc.scalar.activation(out=msin_t[:], in_=frac[:], func=ACT.Sin, scale=-two_pi)
             nc.scalar.activation(out=sin_t[:], in_=frac[:], func=ACT.Sin, scale=two_pi)
-            nc.gpsimd.tensor_tensor(out=tb[:, a0:a1, 0, :], in0=msin_t[:], in1=tb[:, a0:a1, 2, :], op=ALU.subtract)
-            nc.gpsimd.tensor_tensor(out=tb[:, a0:a1, 1, :], in0=sin_t[:], in1=tb[:, a0:a1, 2, :], op=ALU.subtract)
+            for a in range(a0, a1, 2):
+                nc.gpsimd.tensor_tensor(out=tb[:, a : a + 2, 0, :], in0=msin_t[:, a - a0 : a - a0 + 2], in1=tb[:, a : a + 2, 2, :], op=ALU.subtract)
+                nc.gpsimd.tensor_tensor(out=tb[:, a : a + 2, 1, :], in0=sin_t[:, a - a0 : a - a0 + 2], in1=tb[:, a : a + 2, 2, :], op=ALU.subtract)
 
         make_tables(0, 2)
         make_tables(2, NT)
@@ -111,18 +112,23 @@ def tile_gemma2attention_pa_kernel(tc, x, Wq_bytes, Wq_scale, Wk, out_0, out_1):
         x_codes = keep.tile([P, NT, NG * P], U32, name="x_codes", align_bytes=64)
         x_scales = keep.tile([P, NT, NG * P], U8, name="x_scales", align_bytes=64)
 
-        def prep_x(a):
+        x_grouped = {}
+
+        def prep_x_copy(a):
             words = x_sb[a][:].bitcast(F32)
-            xt = psum.tile([P, NG, 2, P], F32, name="xt", tag="xt", bufs=2)
+            xt = psum.tile([P, NG, 2, P], F32, name="xt", tag="aux", bufs=3)
             for g in range(NG):
                 for u in range(2):
                     nc.tensor.transpose(xt[:, g, u, :], words[:, 256 * g + u : 256 * (g + 1) : 2], ident[:])
-            xg = stage.tile([P, NG, P, 4], BF16, name="xg", tag="xg", bufs=3, align_bytes=64)
-            nc.scalar.copy(out=xg[:].bitcast(F32), in_=xt[:].rearrange("p g u r -> p g r u"))
+            if a % 2 == 0:
+                x_grouped[a // 2] = stage.tile([P, 2, NG, P, 4], BF16, name="xg", tag="xg", bufs=NT // 2, align_bytes=64)
+            nc.scalar.copy(out=x_grouped[a // 2][:, a % 2].bitcast(F32), in_=xt[:].rearrange("p g u r -> p g r u"))
+
+        def prep_x_quant(a0):
             nc.vector.quantize_mx(
-                out=x_codes[:, a, :].bitcast(FP8X4),
-                scales=x_scales[:, a, :],
-                in_=xg[:].rearrange("p g r j -> p (g r j)"),
+                out=x_codes[:, a0 : a0 + 2, :].rearrange("p a c -> p (a c)").bitcast(FP8X4),
+                scales=x_scales[:, a0 : a0 + 2, :].rearrange("p a c -> p (a c)"),
+                in_=x_grouped[a0 // 2][:].rearrange("p a g r j -> p (a g r j)"),
             )
 
         w_codes = {}
@@ -177,60 +183,80 @@ def tile_gemma2attention_pa_kernel(tc, x, Wq_bytes, Wq_scale, Wk, out_0, out_1):
                 stop=stop,
             )
 
-        def rope(j, a0, count, add_engine):
+        sums = {}
+
+        def side_products(j, a0, side):
             kind, n0 = CHUNKS[j]
             table = tb if kind == "k" else tbq
-            dst = out_1 if kind == "k" else out_0
-            side = work.tile([P, 2, width], F32, name="side", tag="side", bufs=3)
-            mid = work.tile([P, 2, half_w], F32, name="mid", tag="mid", bufs=3)
-            res = work.tile([P, 2, width], F32, name="res", tag="res", bufs=6)
-            both = psum.tile([P, 2, half_w], F32, name="both", tag="both", bufs=2)
-            for b in range(count):
+            both = psum.tile([P, 2, half_w], F32, name="both", tag="aux", bufs=3)
+            sums[a0] = both
+            for b in range(2):
                 a = a0 + b
-                acc = psum.tile([P, width], F32, name="acc", tag="acc", bufs=4)
+                acc = psum.tile([P, width], F32, name="acc", tag="acc", bufs=5)
                 for g in range(NG):
                     mx(acc[:], j, a, g, 0, width, g == 0, g == NG - 1)
                 for g in range(NG):
                     for e in range(2):
                         mx(both[:, b, :], j, a, g, e * half_w, (e + 1) * half_w, g == 0 and e == 0, g == NG - 1 and e == 1)
                 nc.vector.tensor_tensor(
-                    out=side[:, b, :].rearrange("p (h i e) -> p h i e", h=CH, e=2),
+                    out=side[:, a, :].rearrange("p (h i e) -> p h i e", h=CH, e=2),
                     in0=table[:, a, 0:2, :].rearrange("p e i -> p i e").unsqueeze(1).to_broadcast([P, CH, HALF, 2]),
                     in1=acc[:].rearrange("p (e h i) -> p h i e", e=2, h=CH),
                     op=ALU.mult,
                 )
+
+        def mid_product(j, a0, mid):
+            kind, n0 = CHUNKS[j]
+            table = tb if kind == "k" else tbq
             nc.vector.tensor_tensor(
-                out=mid[:, 0:count, :].rearrange("p b (h i) -> p b h i", h=CH),
-                in0=table[:, a0 : a0 + count, 2, :].unsqueeze(2).to_broadcast([P, count, CH, HALF]),
-                in1=both[:, 0:count, :].rearrange("p b (h i) -> p b h i", h=CH),
+                out=mid[:, a0 : a0 + 2, :].rearrange("p b (h i) -> p b h i", h=CH),
+                in0=table[:, a0 : a0 + 2, 2, :].unsqueeze(2).to_broadcast([P, 2, CH, HALF]),
+                in1=sums[a0][:].rearrange("p b (h i) -> p b h i", h=CH),
                 op=ALU.mult,
             )
-            add_engine.tensor_tensor(
-                out=res[:, 0:count, :].rearrange("p b (c e) -> p (b c) e", e=2),
-                in0=side[:, 0:count, :].rearrange("p b (c e) -> p (b c) e", e=2),
-                in1=mid[:, 0:count, :].rearrange("p b c -> p (b c)").unsqueeze(2).to_broadcast([P, count * half_w, 2]),
+
+        def finish(j, a0, a1, side, mid, engine):
+            kind, n0 = CHUNKS[j]
+            dst = out_1 if kind == "k" else out_0
+            pairs = side[:, a0:a1, :].rearrange("p b (c e) -> p (b c) e", e=2)
+            engine.tensor_tensor(
+                out=pairs,
+                in0=pairs,
+                in1=mid[:, a0:a1, :].rearrange("p b c -> p (b c)").unsqueeze(2).to_broadcast([P, (a1 - a0) * half_w, 2]),
                 op=ALU.add,
             )
             nc.sync.dma_start(
-                out=dst[0, a0 * P : (a0 + count) * P, n0 : n0 + CH, :].rearrange("(b p) h c -> p b (h c)", p=P),
-                in_=res[:, 0:count, :],
+                out=dst[0, a0 * P : a1 * P, n0 : n0 + CH, :].rearrange("(b p) h c -> p b (h c)", p=P),
+                in_=side[:, a0:a1, :],
             )
 
         prep_w_copy(0, True)
         prep_w_quant(0)
         for a in range(NT):
-            prep_x(a)
+            prep_x_copy(a)
         prep_w_copy(1, False)
         nc.scalar.mul(tbq[:], tb[:], 1.0 / math.sqrt(H))
         last = len(CHUNKS) - 1
         for j in range(len(CHUNKS)):
+            side = work.tile([P, NT, width], F32, name="side", tag="side", bufs=2)
+            mid = work.tile([P, NT, half_w], F32, name="mid", tag="mid", bufs=2)
+            if j + 2 <= last:
+                prep_w_copy(j + 2, False)
             for a0 in range(0, NT, 2):
-                if j == last and a0 == NT - 2:
-                    rope(j, a0, 1, nc.gpsimd)
-                    rope(j, a0 + 1, 1, nc.vector)
-                else:
-                    rope(j, a0, 2, nc.gpsimd)
-                if a0 == 0 and j + 2 < len(CHUNKS):
-                    prep_w_copy(j + 2, False)
-                if a0 == 4 and j + 1 < len(CHUNKS):
+                if j == 0 and a0 % 4 == 0:
+                    prep_x_quant(a0)
+                    prep_x_quant(a0 + 2)
+                side_products(j, a0, side)
+                if a0 == 2 and j < last:
                     prep_w_quant(j + 1)
+                    finish(j, 0, 2, side, mid, nc.vector)
+                mid_product(j, a0, mid)
+                if j == 0 and a0 == 2:
+                    finish(j, 2, 4, side, mid, nc.vector)
+                elif j == last and a0 < 4:
+                    finish(j, a0, a0 + 2, side, mid, nc.gpsimd)
+                elif j < last and a0 > 0:
+                    finish(j, a0, a0 + 2, side, mid, nc.gpsimd)
+            if j == last:
+                finish(j, 4, 6, side, mid, nc.vector)
+                finish(j, 6, NT, side, mid, nc.vector)

@@ -237,9 +237,11 @@ def tile_gemma2attention_pa_kernel(tc, x, Wq_bytes, Wq_scale, Wk, out_0, out_1):
         prep_w_copy(1, False)
         nc.scalar.mul(tbq[:], tb[:], 1.0 / math.sqrt(H))
         last = len(CHUNKS) - 1
+        held = {}
         for j in range(len(CHUNKS)):
             side = work.tile([P, NT, width], F32, name="side", tag="side", bufs=2)
             mid = work.tile([P, NT, half_w], F32, name="mid", tag="mid", bufs=2)
+            held[j] = (side, mid)
             if j + 2 <= last:
                 prep_w_copy(j + 2, False)
             for a0 in range(0, NT, 2):
@@ -247,16 +249,19 @@ def tile_gemma2attention_pa_kernel(tc, x, Wq_bytes, Wq_scale, Wk, out_0, out_1):
                     prep_x_quant(a0)
                     prep_x_quant(a0 + 2)
                 side_products(j, a0, side)
-                if a0 == 2 and j < last:
+                if (a0 == 2 and 0 < j < last) or (a0 == 4 and j == 0):
                     prep_w_quant(j + 1)
+                if a0 == 2:
+                    if j > 0:
+                        finish(j - 1, NT - 1, NT, held[j - 1][0], held[j - 1][1], nc.vector)
                     finish(j, 0, 2, side, mid, nc.vector)
                 mid_product(j, a0, mid)
                 if j == 0 and a0 == 2:
                     finish(j, 2, 4, side, mid, nc.vector)
-                elif j == last and a0 < 4:
+                elif a0 == 2 or (a0 == 4 and j < last):
                     finish(j, a0, a0 + 2, side, mid, nc.gpsimd)
-                elif j < last and a0 > 0:
-                    finish(j, a0, a0 + 2, side, mid, nc.gpsimd)
-            if j == last:
-                finish(j, 4, 6, side, mid, nc.vector)
-                finish(j, 6, NT, side, mid, nc.vector)
+                elif a0 == 6 and j < last:
+                    finish(j, 6, 7, side, mid, nc.gpsimd)
+        finish(last, 4, 6, held[last][0], held[last][1], nc.vector)
+        finish(last, 6, 7, held[last][0], held[last][1], nc.vector)
+        finish(last, 7, NT, held[last][0], held[last][1], nc.vector)

@@ -82,14 +82,13 @@ def tile_gemma2attention_pa_kernel(tc, x, Wq_bytes, Wq_scale, Wk, out_0, out_1):
         tbq = keep.tile([P, NT, 3, HALF], F32, name="tbq")
         two_pi = 2.0 * math.pi
 
-        def make_tables(a0, a1):
+        tmp = {}
+
+        def tables_v(a0, a1):
             n = a1 - a0
             turns = keep.tile([P, n, HALF], F32, name="turns%d" % a0)
             whole = keep.tile([P, n, HALF], I32, name="whole%d" % a0)
             frac = keep.tile([P, n, HALF], F32, name="frac%d" % a0)
-            afrac = keep.tile([P, n, HALF], F32, name="afrac%d" % a0)
-            sin_t = keep.tile([P, n, HALF], F32, name="sin_t%d" % a0)
-            msin_t = keep.tile([P, n, HALF], F32, name="msin_t%d" % a0)
             nc.vector.tensor_tensor(
                 out=turns[:],
                 in0=freq[:].unsqueeze(1).to_broadcast([P, n, HALF]),
@@ -98,16 +97,24 @@ def tile_gemma2attention_pa_kernel(tc, x, Wq_bytes, Wq_scale, Wk, out_0, out_1):
             )
             nc.vector.tensor_copy(out=whole[:], in_=turns[:])
             nc.vector.tensor_tensor(out=frac[:], in0=turns[:], in1=whole[:], op=ALU.subtract)
-            nc.scalar.activation(out=afrac[:], in_=frac[:], func=ACT.Abs)
-            nc.scalar.activation(out=tb[:, a0:a1, 2, :], in_=afrac[:], func=ACT.Sin, scale=-two_pi, bias=math.pi / 2.0)
-            nc.scalar.activation(out=msin_t[:], in_=frac[:], func=ACT.Sin, scale=-two_pi)
-            nc.scalar.activation(out=sin_t[:], in_=frac[:], func=ACT.Sin, scale=two_pi)
-            for a in range(a0, a1, 2):
-                nc.gpsimd.tensor_tensor(out=tb[:, a : a + 2, 0, :], in0=msin_t[:, a - a0 : a - a0 + 2], in1=tb[:, a : a + 2, 2, :], op=ALU.subtract)
-                nc.gpsimd.tensor_tensor(out=tb[:, a : a + 2, 1, :], in0=sin_t[:, a - a0 : a - a0 + 2], in1=tb[:, a : a + 2, 2, :], op=ALU.subtract)
+            afrac = keep.tile([P, n, HALF], F32, name="afrac%d" % a0)
+            sin_t = keep.tile([P, n, HALF], F32, name="sin_t%d" % a0)
+            msin_t = keep.tile([P, n, HALF], F32, name="msin_t%d" % a0)
+            tmp[a0] = (frac, afrac, sin_t, msin_t)
 
-        make_tables(0, 2)
-        make_tables(2, NT)
+        def tables_s(base, a0, a1):
+            frac, afrac, sin_t, msin_t = tmp[base]
+            r = slice(a0 - base, a1 - base)
+            nc.scalar.activation(out=afrac[:, r], in_=frac[:, r], func=ACT.Abs)
+            nc.scalar.activation(out=tb[:, a0:a1, 2, :], in_=afrac[:, r], func=ACT.Sin, scale=-two_pi, bias=math.pi / 2.0)
+            nc.scalar.activation(out=msin_t[:, r], in_=frac[:, r], func=ACT.Sin, scale=-two_pi)
+            nc.scalar.activation(out=sin_t[:, r], in_=frac[:, r], func=ACT.Sin, scale=two_pi)
+
+        def tables_sub(base, a0, a1, engine):
+            frac, afrac, sin_t, msin_t = tmp[base]
+            r = slice(a0 - base, a1 - base)
+            engine.tensor_tensor(out=tb[:, a0:a1, 0, :], in0=msin_t[:, r], in1=tb[:, a0:a1, 2, :], op=ALU.subtract)
+            engine.tensor_tensor(out=tb[:, a0:a1, 1, :], in0=sin_t[:, r], in1=tb[:, a0:a1, 2, :], op=ALU.subtract)
 
         x_codes = keep.tile([P, NT, NG * P], U32, name="x_codes", align_bytes=64)
         x_scales = keep.tile([P, NT, NG * P], U8, name="x_scales", align_bytes=64)
@@ -230,12 +237,16 @@ def tile_gemma2attention_pa_kernel(tc, x, Wq_bytes, Wq_scale, Wk, out_0, out_1):
                 in_=side[:, a0:a1, :],
             )
 
+        tables_v(0, 2)
+        tables_s(0, 0, 2)
+        tables_v(2, NT)
+        tables_s(2, 2, NT)
         prep_w_copy(0, True)
+        tables_sub(0, 0, 2, nc.vector)
         prep_w_quant(0)
         for a in range(NT):
             prep_x_copy(a)
         prep_w_copy(1, False)
-        nc.scalar.mul(tbq[:], tb[:], 1.0 / math.sqrt(H))
         last = len(CHUNKS) - 1
         held = {}
         for j in range(len(CHUNKS)):
@@ -248,6 +259,9 @@ def tile_gemma2attention_pa_kernel(tc, x, Wq_bytes, Wq_scale, Wk, out_0, out_1):
                 if j == 0 and a0 % 4 == 0:
                     prep_x_quant(a0)
                     prep_x_quant(a0 + 2)
+                    if a0 == 0:
+                        tables_sub(2, 2, NT, nc.vector)
+                        nc.scalar.mul(tbq[:], tb[:], 1.0 / math.sqrt(H))
                 side_products(j, a0, side)
                 if (a0 == 2 and 0 < j < last) or (a0 == 4 and j == 0):
                     prep_w_quant(j + 1)

@@ -263,19 +263,15 @@ def tile_gemma2attention_pa_kernel(tc, x, Wq_bytes, Wq_scale, Wk, out_0, out_1):
                         tables_sub(2, 2, NT, nc.vector)
                         nc.scalar.mul(tbq[:], tb[:], 1.0 / math.sqrt(H))
                 side_products(j, a0, side)
-                if (a0 == 2 and 0 < j < last) or (a0 == 4 and j == 0):
-                    prep_w_quant(j + 1)
-                if a0 == 2:
-                    if j > 0:
-                        finish(j - 1, NT - 1, NT, held[j - 1][0], held[j - 1][1], nc.vector)
-                    finish(j, 0, 2, side, mid, nc.vector)
+                if a0 == 4:
+                    if j < last:
+                        prep_w_quant(j + 1)
+                    finish(j, 1, 4, side, mid, nc.vector)
                 mid_product(j, a0, mid)
-                if j == 0 and a0 == 2:
-                    finish(j, 2, 4, side, mid, nc.vector)
-                elif a0 == 2 or (a0 == 4 and j < last):
+                if a0 == 0:
+                    finish(j, 0, 1, side, mid, nc.gpsimd)
+                elif a0 >= 4 and j < last:
                     finish(j, a0, a0 + 2, side, mid, nc.gpsimd)
-                elif a0 == 6 and j < last:
-                    finish(j, 6, 7, side, mid, nc.gpsimd)
         finish(last, 4, 6, held[last][0], held[last][1], nc.vector)
         finish(last, 6, 7, held[last][0], held[last][1], nc.vector)
         finish(last, 7, NT, held[last][0], held[last][1], nc.vector)

@@ -256,22 +256,25 @@ def tile_gemma2attention_pa_kernel(tc, x, Wq_bytes, Wq_scale, Wk, out_0, out_1):
             if j + 2 <= last:
                 prep_w_copy(j + 2, False)
             for a0 in range(0, NT, 2):
-                if j == 0 and a0 % 4 == 0:
-                    prep_x_quant(a0)
-                    prep_x_quant(a0 + 2)
+                if j == 0 and a0 == 0:
+                    prep_x_quant(0)
+                    prep_x_quant(2)
                     if a0 == 0:
                         tables_sub(2, 2, NT, nc.vector)
                         nc.scalar.mul(tbq[:], tb[:], 1.0 / math.sqrt(H))
                 side_products(j, a0, side)
-                if a0 == 4:
-                    if j < last:
-                        prep_w_quant(j + 1)
-                    finish(j, 1, 4, side, mid, nc.vector)
+                if j == 0 and a0 == 0:
+                    prep_x_quant(4)
+                    prep_x_quant(6)
+                if a0 == 4 and j < last:
+                    prep_w_quant(j + 1)
+                    finish(j, 2 if j == 0 else 1, 4, side, mid, nc.vector)
                 mid_product(j, a0, mid)
                 if a0 == 0:
-                    finish(j, 0, 1, side, mid, nc.gpsimd)
+                    finish(j, 0, 1 if 0 < j < last else 2, side, mid, nc.gpsimd)
                 elif a0 >= 4 and j < last:
                     finish(j, a0, a0 + 2, side, mid, nc.gpsimd)
+        finish(last, 2, 4, held[last][0], held[last][1], nc.vector)
         finish(last, 4, 6, held[last][0], held[last][1], nc.vector)
         finish(last, 6, 7, held[last][0], held[last][1], nc.vector)
         finish(last, 7, NT, held[last][0], held[last][1], nc.vector)

@@ -142,6 +142,8 @@ def tile_gemma2attention_pa_kernel(tc, x, Wq_bytes, Wq_scale, Wk, out_0, out_1):
         w_scales = {}
         w_grouped = {}
 
+        late = []
+
         def prep_w_copy(j, on_vector):
             kind, n0 = CHUNKS[j]
             if kind == "k":
@@ -163,6 +165,8 @@ def tile_gemma2attention_pa_kernel(tc, x, Wq_bytes, Wq_scale, Wk, out_0, out_1):
                     view = src[:, g, :, :, e * HALF : (e + 1) * HALF].rearrange("p h t i -> p h i t")
                     if on_vector:
                         nc.vector.tensor_copy(out=wg[:, g, 1 - e], in_=view)
+                    elif j == 1 and 2 * g + e >= 4 - 1:
+                        late.append((wg[:, g, 1 - e], view))
                     else:
                         nc.scalar.copy(out=wg[:, g, 1 - e], in_=view)
             w_grouped[j] = wg
@@ -237,6 +241,29 @@ def tile_gemma2attention_pa_kernel(tc, x, Wq_bytes, Wq_scale, Wk, out_0, out_1):
                 in_=side[:, a0:a1, :],
             )
 
+        def finish_heads(j, u0, u1, side, mid, engine):
+            kind, n0 = CHUNKS[j]
+            dst = out_1 if kind == "k" else out_0
+            pairs = side[:].rearrange("p b (c e) -> p (b c) e", e=2)[:, u0 * HALF : u1 * HALF, :]
+            engine.tensor_tensor(
+                out=pairs,
+                in0=pairs,
+                in1=mid[:].rearrange("p b c -> p (b c)")[:, u0 * HALF : u1 * HALF].unsqueeze(2).to_broadcast([P, (u1 - u0) * HALF, 2]),
+                op=ALU.add,
+            )
+            if u0 % CH:
+                a = u0 // CH
+                nc.sync.dma_start(out=dst[0, a * P : (a + 1) * P, n0 + 1, :], in_=side[:, a, H:])
+            if u1 % CH:
+                a = u1 // CH
+                nc.sync.dma_start(out=dst[0, a * P : (a + 1) * P, n0, :], in_=side[:, a, :H])
+            a0, a1 = (u0 + 1) // CH, u1 // CH
+            if a1 > a0:
+                nc.sync.dma_start(
+                    out=dst[0, a0 * P : a1 * P, n0 : n0 + CH, :].rearrange("(b p) h c -> p b (h c)", p=P),
+                    in_=side[:, a0:a1, :],
+                )
+
         tables_v(0, 2)
         tables_s(0, 0, 2)
         tables_v(2, NT)
@@ -267,11 +294,14 @@ def tile_gemma2attention_pa_kernel(tc, x, Wq_bytes, Wq_scale, Wk, out_0, out_1):
                     prep_x_quant(4)
                     prep_x_quant(6)
                 if a0 == 4 and j < last:
+                    if j == 0:
+                        for dst_ap, src_ap in late:
+                            nc.vector.tensor_copy(out=dst_ap, in_=src_ap)
                     prep_w_quant(j + 1)
-                    finish(j, 2 if j == 0 else 1, 4, side, mid, nc.vector)
+                    finish_heads(j, 4 if j == 0 else 1, 8, side, mid, nc.vector)
                 mid_product(j, a0, mid)
                 if a0 == 0:
-                    finish(j, 0, 1 if 0 < j < last else 2, side, mid, nc.gpsimd)
+                    finish_heads(j, 0, 1 if 0 < j < last else 4, side, mid, nc.gpsimd)
                 elif a0 >= 4 and j < last:
                     finish(j, a0, a0 + 2, side, mid, nc.gpsimd)
         finish(last, 2, 4, held[last][0], held[last][1], nc.vector)

@@ -162,13 +162,15 @@ def tile_gemma2attention_pa_kernel(tc, x, Wq_bytes, Wq_scale, Wk, out_0, out_1):
             wg = stage.tile([P, NG, 2, CH, HALF, 4], BF16, name="wg", tag="wg", bufs=2, align_bytes=64)
             for g in range(NG):
                 for e in range(2):
-                    view = src[:, g, :, :, e * HALF : (e + 1) * HALF].rearrange("p h t i -> p h i t")
-                    if on_vector:
-                        nc.vector.tensor_copy(out=wg[:, g, 1 - e], in_=view)
-                    elif j == 1 and 2 * g + e >= 4 - 1:
-                        late.append((wg[:, g, 1 - e], view))
-                    else:
-                        nc.scalar.copy(out=wg[:, g, 1 - e], in_=view)
+                    for h in range(CH):
+                        view = src[:, g, h, :, e * HALF : (e + 1) * HALF].rearrange("p t (c i) -> p c t i", i=4)
+                        dest = wg[:, g, 1 - e, h].rearrange("p (c i) t -> p c t i", i=4)
+                        if on_vector:
+                            nc.vector.tensor_copy(out=dest, in_=view)
+                        elif j == 1 and 2 * g + e >= 4 - 1:
+                            late.append((dest, view))
+                        else:
+                            nc.scalar.copy(out=dest, in_=view)
             w_grouped[j] = wg
 
         def prep_w_quant(j):

@@ -68,6 +68,8 @@ def tile_gemma2attention_pa_kernel(tc, x, Wq_bytes, Wq_scale, Wk, out_0, out_1):
         nc.gpsimd.iota(tok_i[:], pattern=[[P, NT]], base=0, channel_multiplier=1)
         ident = keep.tile([P, P], F32, name="ident")
         make_identity(nc, ident[:])
+        qscale = keep.tile([P, NG, 4], F32, name="qscale")
+        nc.gpsimd.tensor_scalar(out=qscale[:], in0=wscale[:], scalar1=1.0 / math.sqrt(H), scalar2=None, op0=ALU.mult)
         tok_f = keep.tile([P, NT], F32, name="tok_f")
         nc.vector.tensor_copy(out=tok_f[:], in_=tok_i[:])
 
@@ -79,7 +81,6 @@ def tile_gemma2attention_pa_kernel(tc, x, Wq_bytes, Wq_scale, Wk, out_0, out_1):
             nc.vector.tensor_scalar(out=sel, in0=sel, scalar1=10000.0 ** (-(2.0**b) / HALF), scalar2=None, op0=ALU.mult)
 
         tb = keep.tile([P, NT, 3, HALF], F32, name="tb")
-        tbq = keep.tile([P, NT, 3, HALF], F32, name="tbq")
         two_pi = 2.0 * math.pi
 
         tmp = {}
@@ -99,21 +100,21 @@ def tile_gemma2attention_pa_kernel(tc, x, Wq_bytes, Wq_scale, Wk, out_0, out_1):
             nc.vector.tensor_tensor(out=frac[:], in0=turns[:], in1=whole[:], op=ALU.subtract)
             afrac = keep.tile([P, n, HALF], F32, name="afrac%d" % a0)
             sin_t = keep.tile([P, n, HALF], F32, name="sin_t%d" % a0)
-            msin_t = keep.tile([P, n, HALF], F32, name="msin_t%d" % a0)
-            tmp[a0] = (frac, afrac, sin_t, msin_t)
+            tmp[a0] = (frac, afrac, sin_t)
 
         def tables_s(base, a0, a1):
-            frac, afrac, sin_t, msin_t = tmp[base]
+            frac, afrac, sin_t = tmp[base]
             r = slice(a0 - base, a1 - base)
             nc.scalar.activation(out=afrac[:, r], in_=frac[:, r], func=ACT.Abs)
             nc.scalar.activation(out=tb[:, a0:a1, 2, :], in_=afrac[:, r], func=ACT.Sin, scale=-two_pi, bias=math.pi / 2.0)
-            nc.scalar.activation(out=msin_t[:, r], in_=frac[:, r], func=ACT.Sin, scale=-two_pi)
             nc.scalar.activation(out=sin_t[:, r], in_=frac[:, r], func=ACT.Sin, scale=two_pi)
 
         def tables_sub(base, a0, a1, engine):
-            frac, afrac, sin_t, msin_t = tmp[base]
+            frac, afrac, sin_t = tmp[base]
             r = slice(a0 - base, a1 - base)
-            engine.tensor_tensor(out=tb[:, a0:a1, 0, :], in0=msin_t[:, r], in1=tb[:, a0:a1, 2, :], op=ALU.subtract)
+            engine.scalar_tensor_tensor(
+                out=tb[:, a0:a1, 0, :], in0=sin_t[:, r], scalar=-1.0, in1=tb[:, a0:a1, 2, :], op0=ALU.mult, op1=ALU.subtract
+            )
             engine.tensor_tensor(out=tb[:, a0:a1, 1, :], in0=sin_t[:, r], in1=tb[:, a0:a1, 2, :], op=ALU.subtract)
 
         x_codes = keep.tile([P, NT, NG * P], U32, name="x_codes", align_bytes=64)
@@ -157,7 +158,7 @@ def tile_gemma2attention_pa_kernel(tc, x, Wq_bytes, Wq_scale, Wk, out_0, out_1):
                                 out=src[:, g, n, t, :],
                                 in_=raw[j][:, g, n, t, :].bitcast(FP8),
                                 func=ACT.Copy,
-                                scale=wscale[:, g, t : t + 1],
+                                scale=qscale[:, g, t : t + 1],
                             )
             wg = stage.tile([P, NG, 2, CH, HALF, 4], BF16, name="wg", tag="wg", bufs=2, align_bytes=64)
             for g in range(NG):
@@ -199,8 +200,6 @@ def tile_gemma2attention_pa_kernel(tc, x, Wq_bytes, Wq_scale, Wk, out_0, out_1):
         sums = {}
 
         def side_products(j, a0, side):
-            kind, n0 = CHUNKS[j]
-            table = tb if kind == "k" else tbq
             both = psum.tile([P, 2, half_w], F32, name="both", tag="aux", bufs=3)
             sums[a0] = both
             for b in range(2):
@@ -213,17 +212,15 @@ def tile_gemma2attention_pa_kernel(tc, x, Wq_bytes, Wq_scale, Wk, out_0, out_1):
                         mx(both[:, b, :], j, a, g, e * half_w, (e + 1) * half_w, g == 0 and e == 0, g == NG - 1 and e == 1)
                 nc.vector.tensor_tensor(
                     out=side[:, a, :].rearrange("p (h i e) -> p h i e", h=CH, e=2),
-                    in0=table[:, a, 0:2, :].rearrange("p e i -> p i e").unsqueeze(1).to_broadcast([P, CH, HALF, 2]),
+                    in0=tb[:, a, 0:2, :].rearrange("p e i -> p i e").unsqueeze(1).to_broadcast([P, CH, HALF, 2]),
                     in1=acc[:].rearrange("p (e h i) -> p h i e", e=2, h=CH),
                     op=ALU.mult,
                 )
 
         def mid_product(j, a0, mid):
-            kind, n0 = CHUNKS[j]
-            table = tb if kind == "k" else tbq
             nc.vector.tensor_tensor(
                 out=mid[:, a0 : a0 + 2, :].rearrange("p b (h i) -> p b h i", h=CH),
-                in0=table[:, a0 : a0 + 2, 2, :].unsqueeze(2).to_broadcast([P, 2, CH, HALF]),
+                in0=tb[:, a0 : a0 + 2, 2, :].unsqueeze(2).to_broadcast([P, 2, CH, HALF]),
                 in1=sums[a0][:].rearrange("p b (h i) -> p b h i", h=CH),
                 op=ALU.mult,
             )
@@ -290,7 +287,6 @@ def tile_gemma2attention_pa_kernel(tc, x, Wq_bytes, Wq_scale, Wk, out_0, out_1):
                     prep_x_quant(2)
                     if a0 == 0:
                         tables_sub(2, 2, NT, nc.vector)
-                        nc.scalar.mul(tbq[:], tb[:], 1.0 / math.sqrt(H))
                 side_products(j, a0, side)
                 if j == 0 and a0 == 0:
                     prep_x_quant(4)

@@ -23,6 +23,7 @@ NT = S_LEN // P
 NG = D // 512
 CH = 2
 CHUNKS = (("k", 0), ("k", 2), ("q", 0), ("q", 2), ("q", 4), ("q", 6))
+REDUCE = min(i for i in range(0, HALF + 1, 8) if (S_LEN - 1) * 10000.0 ** (-i / HALF) <= math.pi)
 
 
 def tile_gemma2attention_pa_kernel(tc, x, Wq_bytes, Wq_scale, Wk, out_0, out_1):
@@ -71,43 +72,60 @@ def tile_gemma2attention_pa_kernel(tc, x, Wq_bytes, Wq_scale, Wk, out_0, out_1):
         qscale = keep.tile([P, NG, 4], F32, name="qscale")
         nc.gpsimd.tensor_scalar(out=qscale[:], in0=wscale[:], scalar1=1.0 / math.sqrt(H), scalar2=None, op0=ALU.mult)
         tok_f = keep.tile([P, NT], F32, name="tok_f")
-        nc.vector.tensor_copy(out=tok_f[:], in_=tok_i[:])
-
+        f_lo = keep.tile([P, 16], F32, name="f_lo")
+        f_hi = keep.tile([P, HALF // 16], F32, name="f_hi")
+        nc.vector.memset(f_lo[:], 1.0)
+        nc.vector.memset(f_hi[:], 1.0)
+        for b in range(4):
+            for factor, first_bit, bits in ((f_lo, 0, 4), (f_hi, 4, 3)):
+                if b < bits:
+                    sel = factor[:].rearrange("p (a two l) -> p a two l", two=2, l=2**b)[:, :, 1, :]
+                    nc.vector.tensor_scalar(
+                        out=sel, in0=sel, scalar1=10000.0 ** (-(2.0 ** (first_bit + b)) / HALF), scalar2=None, op0=ALU.mult
+                    )
+        nc.vector.tensor_scalar(out=tok_f[:], in0=tok_i[:], scalar1=1.0 / (2.0 * math.pi), scalar2=None, op0=ALU.mult)
         freq = keep.tile([P, HALF], F32, name="freq")
-        nc.vector.memset(freq[:], 1.0)
-        nc.vector.tensor_scalar(out=freq[:], in0=freq[:], scalar1=1.0 / (2.0 * math.pi), scalar2=None, op0=ALU.mult)
-        for b in range(7):
-            sel = freq[:].rearrange("p (a two l) -> p a two l", two=2, l=2**b)[:, :, 1, :]
-            nc.vector.tensor_scalar(out=sel, in0=sel, scalar1=10000.0 ** (-(2.0**b) / HALF), scalar2=None, op0=ALU.mult)
+        nc.vector.tensor_tensor(
+            out=freq[:].rearrange("p (h l) -> p h l", l=16),
+            in0=f_hi[:].unsqueeze(2).to_broadcast([P, HALF // 16, 16]),
+            in1=f_lo[:].unsqueeze(1).to_broadcast([P, HALF // 16, 16]),
+            op=ALU.mult,
+        )
 
         tb = keep.tile([P, NT, 3, HALF], F32, name="tb")
         two_pi = 2.0 * math.pi
 
         tmp = {}
 
-        def tables_v(a0, a1):
+        whole = {}
+
+        def tables_turns(a0, a1):
             n = a1 - a0
-            turns = keep.tile([P, n, HALF], F32, name="turns%d" % a0)
-            whole = keep.tile([P, n, HALF], I32, name="whole%d" % a0)
             frac = keep.tile([P, n, HALF], F32, name="frac%d" % a0)
             nc.vector.tensor_tensor(
-                out=turns[:],
+                out=frac[:],
                 in0=freq[:].unsqueeze(1).to_broadcast([P, n, HALF]),
                 in1=tok_f[:, a0:a1].unsqueeze(2).to_broadcast([P, n, HALF]),
                 op=ALU.mult,
             )
-            nc.vector.tensor_copy(out=whole[:], in_=turns[:])
-            nc.vector.tensor_tensor(out=frac[:], in0=turns[:], in1=whole[:], op=ALU.subtract)
+            whole[a0] = keep.tile([P, n, REDUCE], I32, name="whole%d" % a0)
             afrac = keep.tile([P, n, HALF], F32, name="afrac%d" % a0)
             sin_t = keep.tile([P, n, HALF], F32, name="sin_t%d" % a0)
             tmp[a0] = (frac, afrac, sin_t)
+
+        def tables_whole(a0):
+            nc.vector.tensor_copy(out=whole[a0][:], in_=tmp[a0][0][:, :, :REDUCE])
+
+        def tables_frac(a0):
+            part = tmp[a0][0][:, :, :REDUCE]
+            nc.vector.tensor_tensor(out=part, in0=part, in1=whole[a0][:], op=ALU.subtract)
 
         def tables_s(base, a0, a1):
             frac, afrac, sin_t = tmp[base]
             r = slice(a0 - base, a1 - base)
             nc.scalar.activation(out=afrac[:, r], in_=frac[:, r], func=ACT.Abs)
-            nc.scalar.activation(out=tb[:, a0:a1, 2, :], in_=afrac[:, r], func=ACT.Sin, scale=-two_pi, bias=math.pi / 2.0)
             nc.scalar.activation(out=sin_t[:, r], in_=frac[:, r], func=ACT.Sin, scale=two_pi)
+            nc.scalar.activation(out=tb[:, a0:a1, 2, :], in_=afrac[:, r], func=ACT.Sin, scale=-two_pi, bias=math.pi / 2.0)
 
         def tables_sub(base, a0, a1, engine):
             frac, afrac, sin_t = tmp[base]
@@ -143,8 +161,6 @@ def tile_gemma2attention_pa_kernel(tc, x, Wq_bytes, Wq_scale, Wk, out_0, out_1):
         w_scales = {}
         w_grouped = {}
 
-        late = []
-
         def prep_w_copy(j, on_vector):
             kind, n0 = CHUNKS[j]
             if kind == "k":
@@ -168,8 +184,6 @@ def tile_gemma2attention_pa_kernel(tc, x, Wq_bytes, Wq_scale, Wk, out_0, out_1):
                         dest = wg[:, g, 1 - e, h].rearrange("p (c i) t -> p c t i", i=4)
                         if on_vector:
                             nc.vector.tensor_copy(out=dest, in_=view)
-                        elif j == 1 and 2 * g + e >= 4 - 1:
-                            late.append((dest, view))
                         else:
                             nc.scalar.copy(out=dest, in_=view)
             w_grouped[j] = wg
@@ -263,9 +277,13 @@ def tile_gemma2attention_pa_kernel(tc, x, Wq_bytes, Wq_scale, Wk, out_0, out_1):
                     in_=side[:, a0:a1, :],
                 )
 
-        tables_v(0, 2)
+        tables_turns(0, 2)
+        tables_turns(2, NT)
+        tables_whole(0)
+        tables_whole(2)
+        tables_frac(0)
         tables_s(0, 0, 2)
-        tables_v(2, NT)
+        tables_frac(2)
         tables_s(2, 2, NT)
         prep_w_copy(0, True)
         tables_sub(0, 0, 2, nc.vector)
@@ -292,9 +310,6 @@ def tile_gemma2attention_pa_kernel(tc, x, Wq_bytes, Wq_scale, Wk, out_0, out_1):
                     prep_x_quant(4)
                     prep_x_quant(6)
                 if a0 == 4 and j < last:
-                    if j == 0:
-                        for dst_ap, src_ap in late:
-                            nc.vector.tensor_copy(out=dst_ap, in_=src_ap)
                     prep_w_quant(j + 1)
                     finish_heads(j, 4 if j == 0 else 1, 8, side, mid, nc.vector)
                 mid_product(j, a0, mid)

@@ -33,7 +33,7 @@ def tile_gemma2attention_pa_kernel(tc, x, Wq_bytes, Wq_scale, Wk, out_0, out_1):
         stage = ctx.enter_context(tc.tile_pool(name="stage", bufs=2))
         work = ctx.enter_context(tc.tile_pool(name="work", bufs=4))
         psum = ctx.enter_context(tc.psum_pool(name="psum", bufs=2))
-        ctx.enter_context(tc.manual_schedule(engines={mybir.EngineType.DVE}))
+        ctx.enter_context(tc.manual_schedule(engines={mybir.EngineType.DVE, mybir.EngineType.Activation}))
 
         raw = {}
         for j, (kind, n0) in enumerate(CHUNKS):
@@ -284,11 +284,13 @@ def tile_gemma2attention_pa_kernel(tc, x, Wq_bytes, Wq_scale, Wk, out_0, out_1):
         tables_frac(0)
         tables_s(0, 0, 2)
         tables_frac(2)
-        tables_s(2, 2, NT)
         prep_w_copy(0, True)
         tables_sub(0, 0, 2, nc.vector)
         prep_w_quant(0)
-        for a in range(NT):
+        for a in range(4):
+            prep_x_copy(a)
+        tables_s(2, 2, NT)
+        for a in range(4, NT):
             prep_x_copy(a)
         prep_w_copy(1, False)
         last = len(CHUNKS) - 1
@@ -303,10 +305,9 @@ def tile_gemma2attention_pa_kernel(tc, x, Wq_bytes, Wq_scale, Wk, out_0, out_1):
                 if j == 0 and a0 == 0:
                     prep_x_quant(0)
                     prep_x_quant(2)
-                    if a0 == 0:
-                        tables_sub(2, 2, NT, nc.vector)
                 side_products(j, a0, side)
                 if j == 0 and a0 == 0:
+                    tables_sub(2, 2, NT, nc.vector)
                     prep_x_quant(4)
                     prep_x_quant(6)
                 if a0 == 4 and j < last:

@@ -161,7 +161,7 @@ def tile_gemma2attention_pa_kernel(tc, x, Wq_bytes, Wq_scale, Wk, out_0, out_1):
         w_scales = {}
         w_grouped = {}
 
-        def prep_w_copy(j, on_vector):
+        def prep_w_copy(j, scalar_pieces):
             kind, n0 = CHUNKS[j]
             if kind == "k":
                 src = raw[j]
@@ -182,10 +182,10 @@ def tile_gemma2attention_pa_kernel(tc, x, Wq_bytes, Wq_scale, Wk, out_0, out_1):
                     for h in range(CH):
                         view = src[:, g, h, :, e * HALF : (e + 1) * HALF].rearrange("p t (c i) -> p c t i", i=4)
                         dest = wg[:, g, 1 - e, h].rearrange("p (c i) t -> p c t i", i=4)
-                        if on_vector:
-                            nc.vector.tensor_copy(out=dest, in_=view)
-                        else:
+                        if (g * 2 + e) * CH + h < scalar_pieces:
                             nc.scalar.copy(out=dest, in_=view)
+                        else:
+                            nc.vector.tensor_copy(out=dest, in_=view)
             w_grouped[j] = wg
 
         def prep_w_quant(j):
@@ -216,18 +216,21 @@ def tile_gemma2attention_pa_kernel(tc, x, Wq_bytes, Wq_scale, Wk, out_0, out_1):
         def side_products(j, a0, side):
             both = psum.tile([P, 2, half_w], F32, name="both", tag="aux", bufs=3)
             sums[a0] = both
+            accs = []
             for b in range(2):
-                a = a0 + b
                 acc = psum.tile([P, width], F32, name="acc", tag="acc", bufs=5)
+                accs.append(acc)
                 for g in range(NG):
-                    mx(acc[:], j, a, g, 0, width, g == 0, g == NG - 1)
+                    mx(acc[:], j, a0 + b, g, 0, width, g == 0, g == NG - 1)
+            for b in range(2):
                 for g in range(NG):
                     for e in range(2):
-                        mx(both[:, b, :], j, a, g, e * half_w, (e + 1) * half_w, g == 0 and e == 0, g == NG - 1 and e == 1)
+                        mx(both[:, b, :], j, a0 + b, g, e * half_w, (e + 1) * half_w, g == 0 and e == 0, g == NG - 1 and e == 1)
+            for b in range(2):
                 nc.vector.tensor_tensor(
-                    out=side[:, a, :].rearrange("p (h i e) -> p h i e", h=CH, e=2),
-                    in0=tb[:, a, 0:2, :].rearrange("p e i -> p i e").unsqueeze(1).to_broadcast([P, CH, HALF, 2]),
-                    in1=acc[:].rearrange("p (e h i) -> p h i e", e=2, h=CH),
+                    out=side[:, a0 + b, :].rearrange("p (h i e) -> p h i e", h=CH, e=2),
+                    in0=tb[:, a0 + b, 0:2, :].rearrange("p e i -> p i e").unsqueeze(1).to_broadcast([P, CH, HALF, 2]),
+                    in1=accs[b][:].rearrange("p (e h i) -> p h i e", e=2, h=CH),
                     op=ALU.mult,
                 )
 
@@ -284,7 +287,7 @@ def tile_gemma2attention_pa_kernel(tc, x, Wq_bytes, Wq_scale, Wk, out_0, out_1):
         tables_frac(0)
         tables_s(0, 0, 2)
         tables_frac(2)
-        prep_w_copy(0, True)
+        prep_w_copy(0, 0)
         tables_sub(0, 0, 2, nc.vector)
         prep_w_quant(0)
         for a in range(4):
@@ -292,7 +295,7 @@ def tile_gemma2attention_pa_kernel(tc, x, Wq_bytes, Wq_scale, Wk, out_0, out_1):
         tables_s(2, 2, NT)
         for a in range(4, NT):
             prep_x_copy(a)
-        prep_w_copy(1, False)
+        prep_w_copy(1, 8)
         last = len(CHUNKS) - 1
         held = {}
         for j in range(len(CHUNKS)):
@@ -300,7 +303,7 @@ def tile_gemma2attention_pa_kernel(tc, x, Wq_bytes, Wq_scale, Wk, out_0, out_1):
             mid = work.tile([P, NT, half_w], F32, name="mid", tag="mid", bufs=2)
             held[j] = (side, mid)
             if j + 2 <= last:
-                prep_w_copy(j + 2, False)
+                prep_w_copy(j + 2, 8)
             for a0 in range(0, NT, 2):
                 if j == 0 and a0 == 0:
                     prep_x_quant(0)
@@ -312,11 +315,16 @@ def tile_gemma2attention_pa_kernel(tc, x, Wq_bytes, Wq_scale, Wk, out_0, out_1):
                     prep_x_quant(6)
                 if a0 == 4 and j < last:
                     prep_w_quant(j + 1)
-                    finish_heads(j, 4 if j == 0 else 1, 8, side, mid, nc.vector)
+                    if j == 0:
+                        finish_heads(j, 4, 8, side, mid, nc.vector)
+                    else:
+                        finish_heads(j, 0, 7, side, mid, nc.vector)
                 mid_product(j, a0, mid)
-                if a0 == 0:
-                    finish_heads(j, 0, 1 if 0 < j < last else 4, side, mid, nc.gpsimd)
-                elif a0 >= 4 and j < last:
+                if a0 == 0 and (j == 0 or j == last):
+                    finish_heads(j, 0, 4, side, mid, nc.gpsimd)
+                elif a0 == 4 and j < last:
+                    finish_heads(j, 8 if j == 0 else 7, 12, side, mid, nc.gpsimd)
+                elif a0 == 6 and j < last:
                     finish(j, a0, a0 + 2, side, mid, nc.gpsimd)
         finish(last, 2, 4, held[last][0], held[last][1], nc.vector)
         finish(last, 4, 6, held[last][0], held[last][1], nc.vector)

@@ -318,12 +318,12 @@ def tile_gemma2attention_pa_kernel(tc, x, Wq_bytes, Wq_scale, Wk, out_0, out_1):
                     if j == 0:
                         finish_heads(j, 4, 8, side, mid, nc.vector)
                     else:
-                        finish_heads(j, 0, 7, side, mid, nc.vector)
+                        finish_heads(j, 0, 6, side, mid, nc.vector)
                 mid_product(j, a0, mid)
                 if a0 == 0 and (j == 0 or j == last):
                     finish_heads(j, 0, 4, side, mid, nc.gpsimd)
                 elif a0 == 4 and j < last:
-                    finish_heads(j, 8 if j == 0 else 7, 12, side, mid, nc.gpsimd)
+                    finish_heads(j, 8 if j == 0 else 6, 12, side, mid, nc.gpsimd)
                 elif a0 == 6 and j < last:
                     finish(j, a0, a0 + 2, side, mid, nc.gpsimd)
         finish(last, 2, 4, held[last][0], held[last][1], nc.vector)

@@ -52,12 +52,13 @@ def tile_gemma2attention_pa_kernel(tc, x, Wq_bytes, Wq_scale, Wk, out_0, out_1):
         x_sb = []
         x_view = x[0].rearrange("(a p) k -> a p k", p=P)
         load_w(0)
+        wscale = keep.tile([P, NG, 4], F32, name="wscale")
         for a in range(NT):
             xt_sb = keep.tile([P, D], BF16, name="x_sb%d" % a)
             nc.sync.dma_start(out=xt_sb[:], in_=x_view[a])
             x_sb.append(xt_sb)
-        wscale = keep.tile([P, NG, 4], F32, name="wscale")
-        nc.sync.dma_start(out=wscale[:], in_=Wq_scale.rearrange("o (g p t) z -> p (o g) (t z)", g=NG, p=P, t=4))
+            if a == 3:
+                nc.sync.dma_start(out=wscale[:], in_=Wq_scale.rearrange("o (g p t) z -> p (o g) (t z)", g=NG, p=P, t=4))
         for j in range(1, len(CHUNKS)):
             load_w(j)
 
@@ -70,7 +71,6 @@ def tile_gemma2attention_pa_kernel(tc, x, Wq_bytes, Wq_scale, Wk, out_0, out_1):
         ident = keep.tile([P, P], F32, name="ident")
         make_identity(nc, ident[:])
         qscale = keep.tile([P, NG, 4], F32, name="qscale")
-        nc.gpsimd.tensor_scalar(out=qscale[:], in0=wscale[:], scalar1=1.0 / math.sqrt(H), scalar2=None, op0=ALU.mult)
         tok_f = keep.tile([P, NT], F32, name="tok_f")
         f_lo = keep.tile([P, 16], F32, name="f_lo")
         f_hi = keep.tile([P, HALF // 16], F32, name="f_hi")
@@ -125,15 +125,13 @@ def tile_gemma2attention_pa_kernel(tc, x, Wq_bytes, Wq_scale, Wk, out_0, out_1):
             r = slice(a0 - base, a1 - base)
             nc.scalar.activation(out=afrac[:, r], in_=frac[:, r], func=ACT.Abs)
             nc.scalar.activation(out=sin_t[:, r], in_=frac[:, r], func=ACT.Sin, scale=two_pi)
-            nc.scalar.activation(out=tb[:, a0:a1, 2, :], in_=afrac[:, r], func=ACT.Sin, scale=-two_pi, bias=math.pi / 2.0)
+            nc.scalar.activation(out=tb[:, a0:a1, 2, :], in_=afrac[:, r], func=ACT.Sin, scale=two_pi, bias=-math.pi / 2.0)
 
         def tables_sub(base, a0, a1, engine):
             frac, afrac, sin_t = tmp[base]
             r = slice(a0 - base, a1 - base)
-            engine.scalar_tensor_tensor(
-                out=tb[:, a0:a1, 0, :], in0=sin_t[:, r], scalar=-1.0, in1=tb[:, a0:a1, 2, :], op0=ALU.mult, op1=ALU.subtract
-            )
-            engine.tensor_tensor(out=tb[:, a0:a1, 1, :], in0=sin_t[:, r], in1=tb[:, a0:a1, 2, :], op=ALU.subtract)
+            engine.tensor_tensor(out=tb[:, a0:a1, 0, :], in0=tb[:, a0:a1, 2, :], in1=sin_t[:, r], op=ALU.subtract)
+            engine.tensor_tensor(out=tb[:, a0:a1, 1, :], in0=tb[:, a0:a1, 2, :], in1=sin_t[:, r], op=ALU.add)
 
         x_codes = keep.tile([P, NT, NG * P], U32, name="x_codes", align_bytes=64)
         x_scales = keep.tile([P, NT, NG * P], U8, name="x_scales", align_bytes=64)
@@ -250,7 +248,7 @@ def tile_gemma2attention_pa_kernel(tc, x, Wq_bytes, Wq_scale, Wk, out_0, out_1):
                 out=pairs,
                 in0=pairs,
                 in1=mid[:, a0:a1, :].rearrange("p b c -> p (b c)").unsqueeze(2).to_broadcast([P, (a1 - a0) * half_w, 2]),
-                op=ALU.add,
+                op=ALU.subtract,
             )
             nc.sync.dma_start(
                 out=dst[0, a0 * P : a1 * P, n0 : n0 + CH, :].rearrange("(b p) h c -> p b (h c)", p=P),
@@ -265,7 +263,7 @@ def tile_gemma2attention_pa_kernel(tc, x, Wq_bytes, Wq_scale, Wk, out_0, out_1):
                 out=pairs,
                 in0=pairs,
                 in1=mid[:].rearrange("p b c -> p (b c)")[:, u0 * HALF : u1 * HALF].unsqueeze(2).to_broadcast([P, (u1 - u0) * HALF, 2]),
-                op=ALU.add,
+                op=ALU.subtract,
             )
             if u0 % CH:
                 a = u0 // CH
@@ -290,6 +288,7 @@ def tile_gemma2attention_pa_kernel(tc, x, Wq_bytes, Wq_scale, Wk, out_0, out_1):
         prep_w_copy(0, 0)
         tables_sub(0, 0, 2, nc.vector)
         prep_w_quant(0)
+        nc.vector.tensor_scalar(out=qscale[:], in0=wscale[:], scalar1=1.0 / math.sqrt(H), scalar2=None, op0=ALU.mult)
         for a in range(4):
             prep_x_copy(a)
         tables_s(2, 2, NT)

import math
from contextlib import ExitStack

import concourse.mybir as mybir
from concourse.masks import make_identity

S_LEN, D, NQ, NKV, H = 1024, 1024, 8, 4, 256
HALF = H // 2
FLOPS = 2 * S_LEN * D * (NQ + NKV) * H

F32 = mybir.dt.float32
BF16 = mybir.dt.bfloat16
U32 = mybir.dt.uint32
U8 = mybir.dt.uint8
I32 = mybir.dt.int32
FP8 = mybir.dt.float8_e4m3fn
FP8X4 = mybir.dt.float8_e4m3fn_x4
ALU = mybir.AluOpType
ACT = mybir.ActivationFunctionType

P = 128
NT = S_LEN // P
NG = D // 512
CH = 2
CHUNKS = (("k", 0), ("k", 2), ("q", 0), ("q", 2), ("q", 4), ("q", 6))
REDUCE = min(i for i in range(0, HALF + 1, 8) if (S_LEN - 1) * 10000.0 ** (-i / HALF) <= math.pi)


def tile_gemma2attention_pa_kernel(tc, x, Wq_bytes, Wq_scale, Wk, out_0, out_1):
    nc = tc.nc
    with ExitStack() as ctx:
        keep = ctx.enter_context(tc.tile_pool(name="keep", bufs=1))
        stage = ctx.enter_context(tc.tile_pool(name="stage", bufs=2))
        work = ctx.enter_context(tc.tile_pool(name="work", bufs=4))
        psum = ctx.enter_context(tc.psum_pool(name="psum", bufs=2))
        ctx.enter_context(tc.manual_schedule(engines={mybir.EngineType.DVE, mybir.EngineType.Activation}))

        raw = {}
        for j, (kind, n0) in enumerate(CHUNKS):
            if kind == "k":
                raw[j] = keep.tile([P, NG, CH, 4, H], BF16, name="wk_raw%d" % j)
            else:
                raw[j] = keep.tile([P, NG, CH, 4, H], U8, name="wq_bytes%d" % j)

        def load_w(j):
            kind, n0 = CHUNKS[j]
            src = Wk if kind == "k" else Wq_bytes
            view = src[n0 : n0 + CH].rearrange("n (g p t) c -> g p n (t c)", g=NG, p=P, t=4)
            for g in range(NG):
                nc.sync.dma_start(out=raw[j][:, g].rearrange("p n t c -> p n (t c)"), in_=view[g])

        x_sb = []
        x_view = x[0].rearrange("(a p) k -> a p k", p=P)
        load_w(0)
        wscale = keep.tile([P, NG, 4], F32, name="wscale")
        for a in range(NT):
            xt_sb = keep.tile([P, D], BF16, name="x_sb%d" % a)
            nc.sync.dma_start(out=xt_sb[:], in_=x_view[a])
            x_sb.append(xt_sb)
            if a == 3:
                nc.sync.dma_start(out=wscale[:], in_=Wq_scale.rearrange("o (g p t) z -> p (o g) (t z)", g=NG, p=P, t=4))
        for j in range(1, len(CHUNKS)):
            load_w(j)

        warm = keep.tile([P, 1], F32, name="warm")
        nc.vector.memset(warm[:], 0.0)
        nc.scalar.activation(out=warm[:], in_=warm[:], func=ACT.Sin)

        tok_i = keep.tile([P, NT], I32, name="tok_i")
        nc.gpsimd.iota(tok_i[:], pattern=[[P, NT]], base=0, channel_multiplier=1)
        ident = keep.tile([P, P], F32, name="ident")
        make_identity(nc, ident[:])
        qscale = keep.tile([P, NG, 4], F32, name="qscale")
        tok_f = keep.tile([P, NT], F32, name="tok_f")
        f_lo = keep.tile([P, 16], F32, name="f_lo")
        f_hi = keep.tile([P, HALF // 16], F32, name="f_hi")
        nc.vector.memset(f_lo[:], 1.0)
        nc.vector.memset(f_hi[:], 1.0)
        for b in range(4):
            for factor, first_bit, bits in ((f_lo, 0, 4), (f_hi, 4, 3)):
                if b < bits:
                    sel = factor[:].rearrange("p (a two l) -> p a two l", two=2, l=2**b)[:, :, 1, :]
                    nc.vector.tensor_scalar(
                        out=sel, in0=sel, scalar1=10000.0 ** (-(2.0 ** (first_bit + b)) / HALF), scalar2=None, op0=ALU.mult
                    )
        nc.vector.tensor_scalar(out=tok_f[:], in0=tok_i[:], scalar1=1.0 / (2.0 * math.pi), scalar2=None, op0=ALU.mult)
        freq = keep.tile([P, HALF], F32, name="freq")
        nc.vector.tensor_tensor(
            out=freq[:].rearrange("p (h l) -> p h l", l=16),
            in0=f_hi[:].unsqueeze(2).to_broadcast([P, HALF // 16, 16]),
            in1=f_lo[:].unsqueeze(1).to_broadcast([P, HALF // 16, 16]),
            op=ALU.mult,
        )

        tb = keep.tile([P, NT, 3, HALF], F32, name="tb")
        two_pi = 2.0 * math.pi

        tmp = {}

        whole = {}

        def tables_turns(a0, a1):
            n = a1 - a0
            frac = keep.tile([P, n, HALF], F32, name="frac%d" % a0)
            nc.vector.tensor_tensor(
                out=frac[:],
                in0=freq[:].unsqueeze(1).to_broadcast([P, n, HALF]),
                in1=tok_f[:, a0:a1].unsqueeze(2).to_broadcast([P, n, HALF]),
                op=ALU.mult,
            )
            whole[a0] = keep.tile([P, n, REDUCE], I32, name="whole%d" % a0)
            afrac = keep.tile([P, n, HALF], F32, name="afrac%d" % a0)
            sin_t = keep.tile([P, n, HALF], F32, name="sin_t%d" % a0)
            tmp[a0] = (frac, afrac, sin_t)

        def tables_whole(a0):
            nc.vector.tensor_copy(out=whole[a0][:], in_=tmp[a0][0][:, :, :REDUCE])

        def tables_frac(a0):
            part = tmp[a0][0][:, :, :REDUCE]
            nc.vector.tensor_tensor(out=part, in0=part, in1=whole[a0][:], op=ALU.subtract)

        def tables_s(base, a0, a1):
            frac, afrac, sin_t = tmp[base]
            r = slice(a0 - base, a1 - base)
            nc.scalar.activation(out=afrac[:, r], in_=frac[:, r], func=ACT.Abs)
            nc.scalar.activation(out=sin_t[:, r], in_=frac[:, r], func=ACT.Sin, scale=two_pi)
            nc.scalar.activation(out=tb[:, a0:a1, 2, :], in_=afrac[:, r], func=ACT.Sin, scale=two_pi, bias=-math.pi / 2.0)

        def tables_sub(base, a0, a1, engine):
            frac, afrac, sin_t = tmp[base]
            r = slice(a0 - base, a1 - base)
            engine.tensor_tensor(out=tb[:, a0:a1, 0, :], in0=tb[:, a0:a1, 2, :], in1=sin_t[:, r], op=ALU.subtract)
            engine.tensor_tensor(out=tb[:, a0:a1, 1, :], in0=tb[:, a0:a1, 2, :], in1=sin_t[:, r], op=ALU.add)

        x_codes = keep.tile([P, NT, NG * P], U32, name="x_codes", align_bytes=64)
        x_scales = keep.tile([P, NT, NG * P], U8, name="x_scales", align_bytes=64)

        x_grouped = {}

        def prep_x_copy(a):
            words = x_sb[a][:].bitcast(F32)
            xt = psum.tile([P, NG, 2, P], F32, name="xt", tag="aux", bufs=3)
            for g in range(NG):
                for u in range(2):
                    nc.tensor.transpose(xt[:, g, u, :], words[:, 256 * g + u : 256 * (g + 1) : 2], ident[:])
            if a % 2 == 0:
                x_grouped[a // 2] = stage.tile([P, 2, NG, P, 4], BF16, name="xg", tag="xg", bufs=NT // 2, align_bytes=64)
            nc.scalar.copy(out=x_grouped[a // 2][:, a % 2].bitcast(F32), in_=xt[:].rearrange("p g u r -> p g r u"))

        def prep_x_quant(a0):
            nc.vector.quantize_mx(
                out=x_codes[:, a0 : a0 + 2, :].rearrange("p a c -> p (a c)").bitcast(FP8X4),
                scales=x_scales[:, a0 : a0 + 2, :].rearrange("p a c -> p (a c)"),
                in_=x_grouped[a0 // 2][:].rearrange("p a g r j -> p (a g r j)"),
            )

        w_codes = {}
        w_scales = {}
        w_grouped = {}

        def prep_w_copy(j, scalar_pieces):
            kind, n0 = CHUNKS[j]
            if kind == "k":
                src = raw[j]
            else:
                src = stage.tile([P, NG, CH, 4, H], BF16, name="wide", tag="wide", bufs=2)
                for g in range(NG):
                    for n in range(CH):
                        for t in range(4):
                            nc.scalar.activation(
                                out=src[:, g, n, t, :],
                                in_=raw[j][:, g, n, t, :].bitcast(FP8),
                                func=ACT.Copy,
                                scale=qscale[:, g, t : t + 1],
                            )
            wg = stage.tile([P, NG, 2, CH, HALF, 4], BF16, name="wg", tag="wg", bufs=2, align_bytes=64)
            for g in range(NG):
                for e in range(2):
                    for h in range(CH):
                        view = src[:, g, h, :, e * HALF : (e + 1) * HALF].rearrange("p t (c i) -> p c t i", i=4)
                        dest = wg[:, g, 1 - e, h].rearrange("p (c i) t -> p c t i", i=4)
                        if (g * 2 + e) * CH + h < scalar_pieces:
                            nc.scalar.copy(out=dest, in_=view)
                        else:
                            nc.vector.tensor_copy(out=dest, in_=view)
            w_grouped[j] = wg

        def prep_w_quant(j):
            w_codes[j] = keep.tile([P, NG * CH * H], U32, name="w_codes%d" % j, align_bytes=64)
            w_scales[j] = keep.tile([P, NG * CH * H], U8, name="w_scales%d" % j, align_bytes=64)
            nc.vector.quantize_mx(
                out=w_codes[j][:].bitcast(FP8X4),
                scales=w_scales[j][:],
                in_=w_grouped[j][:].rearrange("p g e h i t -> p (g e h i t)"),
            )

        width = CH * H
        half_w = CH * HALF

        def mx(out, j, a, g, c0, c1, start, stop):
            nc.tensor.matmul_mx(
                out=out,
                lhsT=x_codes[:, a, g * P : (g + 1) * P].bitcast(FP8X4),
                lhsT_scale=x_scales[:, a, g * P : (g + 1) * P],
                rhs=w_codes[j][:, g * width + c0 : g * width + c1].bitcast(FP8X4),
                rhs_scale=w_scales[j][:, g * width + c0 : g * width + c1],
                start=start,
                stop=stop,
            )

        sums = {}

        def side_products(j, a0, side):
            both = psum.tile([P, 2, half_w], F32, name="both", tag="aux", bufs=3)
            sums[a0] = both
            accs = []
            for b in range(2):
                acc = psum.tile([P, width], F32, name="acc", tag="acc", bufs=5)
                accs.append(acc)
                for g in range(NG):
                    mx(acc[:], j, a0 + b, g, 0, width, g == 0, g == NG - 1)
            for b in range(2):
                for g in range(NG):
                    for e in range(2):
                        mx(both[:, b, :], j, a0 + b, g, e * half_w, (e + 1) * half_w, g == 0 and e == 0, g == NG - 1 and e == 1)
            for b in range(2):
                nc.vector.tensor_tensor(
                    out=side[:, a0 + b, :].rearrange("p (h i e) -> p h i e", h=CH, e=2),
                    in0=tb[:, a0 + b, 0:2, :].rearrange("p e i -> p i e").unsqueeze(1).to_broadcast([P, CH, HALF, 2]),
                    in1=accs[b][:].rearrange("p (e h i) -> p h i e", e=2, h=CH),
                    op=ALU.mult,
                )

        def mid_product(j, a0, mid):
            nc.vector.tensor_tensor(
                out=mid[:, a0 : a0 + 2, :].rearrange("p b (h i) -> p b h i", h=CH),
                in0=tb[:, a0 : a0 + 2, 2, :].unsqueeze(2).to_broadcast([P, 2, CH, HALF]),
                in1=sums[a0][:].rearrange("p b (h i) -> p b h i", h=CH),
                op=ALU.mult,
            )

        def finish(j, a0, a1, side, mid, engine):
            kind, n0 = CHUNKS[j]
            dst = out_1 if kind == "k" else out_0
            pairs = side[:, a0:a1, :].rearrange("p b (c e) -> p (b c) e", e=2)
            engine.tensor_tensor(
                out=pairs,
                in0=pairs,
                in1=mid[:, a0:a1, :].rearrange("p b c -> p (b c)").unsqueeze(2).to_broadcast([P, (a1 - a0) * half_w, 2]),
                op=ALU.subtract,
            )
            nc.sync.dma_start(
                out=dst[0, a0 * P : a1 * P, n0 : n0 + CH, :].rearrange("(b p) h c -> p b (h c)", p=P),
                in_=side[:, a0:a1, :],
            )

        def finish_heads(j, u0, u1, side, mid, engine):
            kind, n0 = CHUNKS[j]
            dst = out_1 if kind == "k" else out_0
            pairs = side[:].rearrange("p b (c e) -> p (b c) e", e=2)[:, u0 * HALF : u1 * HALF, :]
            engine.tensor_tensor(
                out=pairs,
                in0=pairs,
                in1=mid[:].rearrange("p b c -> p (b c)")[:, u0 * HALF : u1 * HALF].unsqueeze(2).to_broadcast([P, (u1 - u0) * HALF, 2]),
                op=ALU.subtract,
            )
            if u0 % CH:
                a = u0 // CH
                nc.sync.dma_start(out=dst[0, a * P : (a + 1) * P, n0 + 1, :], in_=side[:, a, H:])
            if u1 % CH:
                a = u1 // CH
                nc.sync.dma_start(out=dst[0, a * P : (a + 1) * P, n0, :], in_=side[:, a, :H])
            a0, a1 = (u0 + 1) // CH, u1 // CH
            if a1 > a0:
                nc.sync.dma_start(
                    out=dst[0, a0 * P : a1 * P, n0 : n0 + CH, :].rearrange("(b p) h c -> p b (h c)", p=P),
                    in_=side[:, a0:a1, :],
                )

        tables_turns(0, 2)
        tables_turns(2, NT)
        tables_whole(0)
        tables_whole(2)
        tables_frac(0)
        tables_s(0, 0, 2)
        tables_frac(2)
        prep_w_copy(0, 0)
        tables_sub(0, 0, 2, nc.vector)
        prep_w_quant(0)
        nc.vector.tensor_scalar(out=qscale[:], in0=wscale[:], scalar1=1.0 / math.sqrt(H), scalar2=None, op0=ALU.mult)
        for a in range(4):
            prep_x_copy(a)
        tables_s(2, 2, NT)
        for a in range(4, NT):
            prep_x_copy(a)
        prep_w_copy(1, 8)
        last = len(CHUNKS) - 1
        held = {}
        for j in range(len(CHUNKS)):
            side = work.tile([P, NT, width], F32, name="side", tag="side", bufs=2)
            mid = work.tile([P, NT, half_w], F32, name="mid", tag="mid", bufs=2)
            held[j] = (side, mid)
            if j + 2 <= last:
                prep_w_copy(j + 2, 8)
            for a0 in range(0, NT, 2):
                if j == 0 and a0 == 0:
                    prep_x_quant(0)
                    prep_x_quant(2)
                side_products(j, a0, side)
                if j == 0 and a0 == 0:
                    tables_sub(2, 2, NT, nc.vector)
                    prep_x_quant(4)
                    prep_x_quant(6)
                if a0 == 4 and j < last:
                    prep_w_quant(j + 1)
                    if j == 0:
                        finish_heads(j, 4, 8, side, mid, nc.vector)
                    else:
                        finish_heads(j, 0, 6, side, mid, nc.vector)
                mid_product(j, a0, mid)
                if a0 == 0 and (j == 0 or j == last):
                    finish_heads(j, 0, 4, side, mid, nc.gpsimd)
                elif a0 == 4 and j < last:
                    finish_heads(j, 8 if j == 0 else 6, 12, side, mid, nc.gpsimd)
                elif a0 == 6 and j < last:
                    finish(j, a0, a0 + 2, side, mid, nc.gpsimd)
        finish(last, 2, 4, held[last][0], held[last][1], nc.vector)
        finish(last, 4, 6, held[last][0], held[last][1], nc.vector)
        finish(last, 6, 7, held[last][0], held[last][1], nc.vector)
        finish(last, 7, NT, held[last][0], held[last][1], nc.vector)
